import numpy as np
import ml_dtypes


def mxq(x, axis, fmt="e4m3"):
    dtype, down = {"e4m3": (ml_dtypes.float8_e4m3fn, 7), "e5m2": (ml_dtypes.float8_e5m2, 14)}[fmt]
    v = np.moveaxis(np.asarray(x, np.float32).astype(ml_dtypes.bfloat16).astype(np.float64), axis, -1)
    blocks = v.reshape(v.shape[:-1] + (-1, 32))
    amax = np.abs(blocks).max(-1, keepdims=True)
    byte = np.maximum(np.where(amax > 0, np.frexp(amax)[1] - 1 + 127, 0) - down, 1)
    scale = np.exp2(byte - 127.0)
    codes = (blocks / scale).astype(np.float32).astype(dtype).astype(np.float64)
    return np.moveaxis((codes * scale).reshape(v.shape), -1, axis)


WIDE = False


def mx_kscale(k):
    if not WIDE:
        return np.ones(k)
    levels = np.array([10, -10, 5, -5, 0])
    a = np.random.permutation(np.resize(levels, k // 512 * 4)).reshape(k // 512, 4)
    idx = np.arange(k)
    return np.exp2(a[idx // 512, idx % 128 // 32])


BF16 = ml_dtypes.bfloat16


def bf(x):
    return np.asarray(x, np.float32).astype(BF16)


def f64(x):
    return np.asarray(x).astype(np.float64)


B, S, D, H, KV, HD, F = 8, 512, 256, 4, 2, 256, 5632
REP = H // KV
NQ = H * HD


def setup_inputs():
    t = mx_kscale(KV * HD).reshape(KV, HD)
    to = np.repeat(t, REP, axis=0).reshape(NQ)
    mask = np.where(np.tril(np.ones((S, S), bool)), np.random.standard_normal((S, S)), -1e9)
    sgn = np.where(np.random.standard_normal((KV, HD)) < 0.0, -1.0, 1.0)
    return {"q_rot": bf(np.random.standard_normal((B, S, H, HD))),
            "k_rot": bf(np.random.standard_normal((B, S, KV, HD))),
            "v": bf((0.25 + np.abs(np.random.standard_normal((B, S, KV, HD)))) * sgn * t),
            "mask": bf(mask),
            "wo": bf(np.random.standard_normal((D, NQ)) * 2.0 / np.sqrt(NQ) / to[None, :]),
            "x": bf(np.random.standard_normal((B, S, D)) * np.random.uniform(0.5, 2.0, (B, S, 1)))}


def reference(q_rot, k_rot, v, mask, wo, x):
    q = f64(q_rot).reshape(B, S, KV, REP, HD).transpose(0, 2, 3, 1, 4).reshape(B, KV, REP * S, HD)
    k = f64(k_rot).transpose(0, 2, 3, 1)
    s = (q @ k / np.sqrt(HD)).reshape(B, KV, REP, S, S) + f64(mask)
    e = np.exp(s - s.max(-1, keepdims=True)).reshape(B, KV, REP * S, S)
    o = (mxq(e, 3, "e4m3") @ mxq(f64(v).transpose(0, 2, 1, 3), 2, "e4m3")) / e.sum(-1, keepdims=True)
    o = o.reshape(B, KV, REP, S, HD).transpose(0, 3, 1, 2, 4).reshape(B, S, NQ)
    return f64(x) + (mxq(o, 2, "e4m3") @ mxq(f64(wo), 1, "e4m3").T)

@@ -1,0 +1,254 @@
+import concourse.mybir as mybir
+from concourse.masks import make_identity
+
+F32 = mybir.dt.float32
+BF16 = mybir.dt.bfloat16
+U32 = mybir.dt.uint32
+U8 = mybir.dt.uint8
+FP8X4 = mybir.dt.float8_e4m3fn_x4
+ACT = mybir.ActivationFunctionType
+ALU = mybir.AluOpType
+AXIS = mybir.AxisListType
+
+B, S, D, H, KV, HD = 8, 512, 256, 4, 2, 256
+REP = H // KV
+NQ = H * HD
+P = 128
+TILES = S // P
+WORDS = HD // 2
+E_SLOTS = 2
+
+FLOPS = 2 * B * H * S * S * HD * 2 + 2 * B * S * NQ * D
+
+
+def tile_transformerblock_pb_t_kernel(tc, q_rot, k_rot, v, mask, wo, x, out):
+    nc = tc.nc
+    with (
+        tc.tile_pool(name="fixed", bufs=1) as fixed,
+        tc.tile_pool(name="batch", bufs=2) as batch,
+        tc.tile_pool(name="head", bufs=2) as head,
+        tc.psum_pool(name="psum_s", bufs=3) as psum_s,
+        tc.psum_pool(name="psum_t", bufs=2) as psum_t,
+        tc.psum_pool(name="psum_pv", bufs=2) as psum_pv,
+        tc.psum_pool(name="psum_out", bufs=1) as psum_out,
+    ):
+        ident_f32 = fixed.tile([P, P], F32)
+        make_identity(nc, ident_f32[:])
+        ident_bf16 = fixed.tile([P, P], BF16)
+        make_identity(nc, ident_bf16[:])
+
+        def transpose_words(bank, sources):
+            for i, words in enumerate(sources):
+                nc.tensor.transpose(bank[:, i * P : (i + 1) * P], words, ident_f32[:])
+
+        def interleave(copy, grouped_words, bank):
+            copy(
+                out=grouped_words.rearrange("p (a c u) -> p a c u", a=2, u=2),
+                in_=bank.rearrange("p (a u c) -> p a c u", a=2, u=2),
+            )
+
+        mask_sb = fixed.tile([P, TILES * S], BF16)
+        nc.sync.dma_start(
+            out=mask_sb[:].rearrange("p (t k) -> p t k", t=TILES),
+            in_=mask.rearrange("(t p) k -> p t k", p=P),
+        )
+
+        wo_sb = fixed.tile([P, (D // P) * NQ], BF16)
+        nc.sync.dma_start(
+            out=wo_sb[:].rearrange("p (t j) -> p t j", t=D // P),
+            in_=wo.rearrange("(t p) j -> p t j", p=P),
+        )
+        wo_words = wo_sb[:].bitcast(F32).rearrange("p (t h w) -> p t h w", t=D // P, h=H)
+        wo_grouped = fixed.tile([P, KV * D * 4], BF16, align_bytes=64)
+        wo_codes = fixed.tile([P, KV * D], U32, align_bytes=64)
+        wo_scales = fixed.tile([P, KV * D], U8, align_bytes=64)
+        for g in range(KV):
+            bank = psum_t.tile([P, 4 * P], F32, tag="bank")
+            transpose_words(bank, [wo_words[:, t, REP * g + u, :] for t in range(D // P) for u in range(REP)])
+            interleave(
+                nc.vector.tensor_copy,
+                wo_grouped[:].bitcast(F32)[:, g * 2 * D : (g + 1) * 2 * D],
+                bank[:],
+            )
+        nc.vector.quantize_mx(out=wo_codes[:].bitcast(FP8X4), scales=wo_scales[:], in_=wo_grouped[:])
+
+        e_tiles = [
+            [fixed.tile([P, S], BF16, name="e_%d_%d" % (slot, t)) for t in range(TILES)]
+            for slot in range(E_SLOTS)
+        ]
+        for slot in range(E_SLOTS):
+            for t in range(TILES - 1):
+                nc.vector.memset(e_tiles[slot][t][:, (t + 1) * P :], 0.0)
+
+        for b in range(B):
+            k_sb = batch.tile([P, TILES * KV * HD], BF16)
+            nc.sync.dma_start(
+                out=k_sb[:].rearrange("p (t c) -> p t c", t=TILES),
+                in_=k_rot[b].rearrange("(t p) g d -> p t (g d)", p=P),
+            )
+            q_sb = batch.tile([P, TILES * NQ], BF16)
+            nc.sync.dma_start(
+                out=q_sb[:].rearrange("p (t c) -> p t c", t=TILES),
+                in_=q_rot[b].rearrange("(t p) h d -> p t (h d)", p=P),
+            )
+            v_sb = batch.tile([P, 4 * KV * HD], BF16)
+            nc.sync.dma_start(
+                out=v_sb[:].rearrange("p (u c) -> p u c", u=2),
+                in_=v[b].rearrange("(u p j) g d -> p u (j g d)", u=2, j=2),
+            )
+            x_sb = batch.tile([P, TILES * D], BF16)
+            nc.sync.dma_start(
+                out=x_sb[:].rearrange("p (t d) -> p t d", t=TILES),
+                in_=x[b].rearrange("(t p) d -> p t d", p=P),
+            )
+
+            v_grouped = batch.tile([P, KV * HD * 4], BF16, align_bytes=64)
+            nc.vector.tensor_copy(
+                out=v_grouped[:].rearrange("p (c i) -> p c i", i=4),
+                in_=v_sb[:].rearrange("p (i c) -> p c i", i=4),
+            )
+            v_codes = batch.tile([P, KV * HD], U32, align_bytes=64)
+            v_scales = batch.tile([P, KV * HD], U8, align_bytes=64)
+            nc.vector.quantize_mx(out=v_codes[:].bitcast(FP8X4), scales=v_scales[:], in_=v_grouped[:])
+
+            nc.vector.tensor_scalar_mul(out=k_sb[:], in0=k_sb[:], scalar1=1.0 / 16.0)
+            k_words = k_sb[:].bitcast(F32).rearrange("p (t g w) -> p t g w", t=TILES, g=KV)
+            q_words = q_sb[:].bitcast(F32).rearrange("p (t h w) -> p t h w", t=TILES, h=H)
+            kT = batch.tile([P, KV * S], F32)
+            qT = batch.tile([P, H * S], F32)
+            for g in range(KV):
+                bank = psum_t.tile([P, 4 * P], F32, tag="bank")
+                transpose_words(bank, [k_words[:, t, g, :] for t in range(TILES)])
+                nc.vector.tensor_copy(out=kT[:, g * S : (g + 1) * S], in_=bank[:])
+            for t in range(TILES):
+                bank = psum_t.tile([P, 4 * P], F32, tag="bank")
+                transpose_words(bank, [q_words[:, t, h, :] for h in range(H)])
+                nc.vector.tensor_copy(
+                    out=qT[:].rearrange("p (h s) -> p h s", h=H)[:, :, t * P : (t + 1) * P],
+                    in_=bank[:].rearrange("p (h s) -> p h s", h=H),
+                )
+            kT_halves = kT[:].bitcast(BF16).rearrange("p (g s j) -> p g s j", g=KV, j=2)
+            qT_halves = qT[:].bitcast(BF16).rearrange("p (h s j) -> p h s j", h=H, j=2)
+
+            o_sb = batch.tile([P, TILES * NQ], BF16)
+            for h in range(H):
+                g = h // REP
+                e_set = e_tiles[h % E_SLOTS]
+                neg_max = head.tile([P, TILES], F32)
+                row_sum = head.tile([P, TILES], F32)
+                for t in range(TILES):
+                    keys = (t + 1) * P
+                    scores = psum_s.tile([P, S], F32)
+                    for j in range(2):
+                        nc.tensor.matmul(
+                            out=scores[:, :keys],
+                            lhsT=qT_halves[:, h, t * P : (t + 1) * P, j],
+                            rhs=kT_halves[:, g, :keys, j],
+                            start=(j == 0),
+                            stop=False,
+                        )
+                    nc.tensor.matmul(
+                        out=scores[:, :keys],
+                        lhsT=ident_bf16[:],
+                        rhs=mask_sb[:, t * S : t * S + keys],
+                        start=False,
+                        stop=True,
+                    )
+                    nc.vector.tensor_reduce(
+                        out=neg_max[:, t : t + 1], in_=scores[:, :keys], axis=AXIS.X, op=ALU.max, negate=True
+                    )
+                    nc.scalar.activation(
+                        out=e_set[t][:, :keys],
+                        in_=scores[:, :keys],
+                        func=ACT.Exp,
+                        bias=neg_max[:, t : t + 1],
+                        accum_out=row_sum[:, t : t + 1],
+                    )
+                inv_sum = head.tile([P, TILES], F32)
+                nc.vector.reciprocal(out=inv_sum[:], in_=row_sum[:])
+
+                e_grouped = head.tile([P, S * 4], BF16, align_bytes=64)
+                for pair in range(TILES // 2):
+                    bank = psum_t.tile([P, 4 * P], F32, tag="bank")
+                    transpose_words(
+                        bank,
+                        [
+                            e_set[2 * pair + a][:].bitcast(F32)[:, u * P : (u + 1) * P]
+                            for a in range(2)
+                            for u in range(2)
+                        ],
+                    )
+                    interleave(
+                        nc.scalar.copy,
+                        e_grouped[:].bitcast(F32)[:, pair * 4 * P : (pair + 1) * 4 * P],
+                        bank[:],
+                    )
+                e_codes = head.tile([P, S], U32, align_bytes=64)
+                e_scales = head.tile([P, S], U8, align_bytes=64)
+                nc.vector.quantize_mx(out=e_codes[:].bitcast(FP8X4), scales=e_scales[:], in_=e_grouped[:])
+
+                for pair in range(TILES // 2):
+                    pv = psum_pv.tile([P, 2 * HD], F32)
+                    for a in range(2):
+                        t = 2 * pair + a
+                        nc.tensor.matmul_mx(
+                            out=pv[:, a * HD : (a + 1) * HD],
+                            lhsT=e_codes[:, t * P : (t + 1) * P].bitcast(FP8X4),
+                            lhsT_scale=e_scales[:, t * P : (t + 1) * P],
+                            rhs=v_codes[:, g * HD : (g + 1) * HD].bitcast(FP8X4),
+                            rhs_scale=v_scales[:, g * HD : (g + 1) * HD],
+                            start=True,
+                            stop=True,
+                        )
+                    for a in range(2):
+                        t = 2 * pair + a
+                        nc.scalar.activation(
+                            out=o_sb[:, t * NQ + h * HD : t * NQ + (h + 1) * HD],
+                            in_=pv[:, a * HD : (a + 1) * HD],
+                            func=ACT.Copy,
+                            scale=inv_sum[:, t : t + 1],
+                        )
+
+            o_words = o_sb[:].bitcast(F32).rearrange("p (t h w) -> p t h w", t=TILES, h=H)
+            o_grouped = batch.tile([P, KV * S * 4], BF16, align_bytes=64)
+            o_codes = batch.tile([P, KV * S], U32, align_bytes=64)
+            o_scales = batch.tile([P, KV * S], U8, align_bytes=64)
+            for g in range(KV):
+                for pair in range(TILES // 2):
+                    bank = psum_t.tile([P, 4 * P], F32, tag="bank")
+                    transpose_words(
+                        bank, [o_words[:, 2 * pair + a, REP * g + u, :] for a in range(2) for u in range(REP)]
+                    )
+                    first = (g * S + pair * 2 * P) * 2
+                    interleave(nc.vector.tensor_copy, o_grouped[:].bitcast(F32)[:, first : first + 4 * P], bank[:])
+                nc.vector.quantize_mx(
+                    out=o_codes[:, g * S : (g + 1) * S].bitcast(FP8X4),
+                    scales=o_scales[:, g * S : (g + 1) * S],
+                    in_=o_grouped[:, g * S * 4 : (g + 1) * S * 4],
+                )
+
+            out_sb = batch.tile([P, TILES * D], F32)
+            for pair in range(TILES // 2):
+                proj = psum_out.tile([P, 2 * D], F32)
+                for a in range(2):
+                    t = 2 * pair + a
+                    for g in range(KV):
+                        nc.tensor.matmul_mx(
+                            out=proj[:, a * D : (a + 1) * D],
+                            lhsT=o_codes[:, g * S + t * P : g * S + (t + 1) * P].bitcast(FP8X4),
+                            lhsT_scale=o_scales[:, g * S + t * P : g * S + (t + 1) * P],
+                            rhs=wo_codes[:, g * D : (g + 1) * D].bitcast(FP8X4),
+                            rhs_scale=wo_scales[:, g * D : (g + 1) * D],
+                            start=(g == 0),
+                            stop=(g == KV - 1),
+                        )
+                nc.vector.tensor_tensor(
+                    out=out_sb[:, pair * 2 * D : (pair + 1) * 2 * D],
+                    in0=proj[:],
+                    in1=x_sb[:, pair * 2 * D : (pair + 1) * 2 * D],
+                    op=ALU.add,
+                )
+            nc.sync.dma_start(
+                out=out[b].rearrange("(t p) d -> p t d", p=P),
+                in_=out_sb[:].rearrange("p (t d) -> p t d", t=TILES),
+            )

@@ -17,6 +17,8 @@ P = 128
 TILES = S // P
 WORDS = HD // 2
 E_SLOTS = 2
+HEADS = B * H
+UNITS = B * KV
 
 FLOPS = 2 * B * H * S * S * HD * 2 + 2 * B * S * NQ * D
 
@@ -25,52 +27,234 @@ def tile_transformerblock_pb_t_kernel(tc, q_rot, k_rot, v, mask, wo, x, out):
     nc = tc.nc
     with (
         tc.tile_pool(name="fixed", bufs=1) as fixed,
-        tc.tile_pool(name="batch", bufs=2) as batch,
-        tc.tile_pool(name="head", bufs=2) as head,
-        tc.psum_pool(name="psum_s", bufs=3) as psum_s,
-        tc.psum_pool(name="psum_t", bufs=2) as psum_t,
-        tc.psum_pool(name="psum_pv", bufs=2) as psum_pv,
-        tc.psum_pool(name="psum_out", bufs=1) as psum_out,
+        tc.tile_pool(name="raw", bufs=2) as raw_pool,
+        tc.tile_pool(name="late", bufs=3) as late_pool,
+        tc.tile_pool(name="unit", bufs=2) as unit_pool,
+        tc.tile_pool(name="long_unit", bufs=4) as long_unit_pool,
+        tc.tile_pool(name="head", bufs=3) as head_pool,
+        tc.tile_pool(name="stats", bufs=4) as stats_pool,
+        tc.psum_pool(name="psum_scores", bufs=3) as psum_scores,
+        tc.psum_pool(name="psum_words", bufs=3) as psum_words,
+        tc.psum_pool(name="psum_mx", bufs=2) as psum_mx,
     ):
         ident_f32 = fixed.tile([P, P], F32)
         make_identity(nc, ident_f32[:])
         ident_bf16 = fixed.tile([P, P], BF16)
         make_identity(nc, ident_bf16[:])
 
-        def transpose_words(bank, sources):
+        def transpose_words(sources):
+            bank = psum_words.tile([P, 4 * P], F32)
             for i, words in enumerate(sources):
                 nc.tensor.transpose(bank[:, i * P : (i + 1) * P], words, ident_f32[:])
+            return bank
 
         def interleave(copy, grouped_words, bank):
             copy(
                 out=grouped_words.rearrange("p (a c u) -> p a c u", a=2, u=2),
-                in_=bank.rearrange("p (a u c) -> p a c u", a=2, u=2),
+                in_=bank[:].rearrange("p (a u c) -> p a c u", a=2, u=2),
             )
 
         mask_sb = fixed.tile([P, TILES * S], BF16)
+
+        raw_of, x_of, kT_of, qT_of, v_of = {}, {}, {}, {}, {}
+        stats_of, e_mx_of, o_of, o_mx_of, out_of = {}, {}, {}, {}, {}
+
+        def load(b):
+            k_sb = raw_pool.tile([P, TILES * KV * HD], BF16)
+            nc.sync.dma_start(
+                out=k_sb[:].rearrange("p (t c) -> p t c", t=TILES),
+                in_=k_rot[b].rearrange("(t p) g d -> p t (g d)", p=P),
+            )
+            q_sb = raw_pool.tile([P, TILES * NQ], BF16)
+            nc.sync.dma_start(
+                out=q_sb[:].rearrange("p (t c) -> p t c", t=TILES),
+                in_=q_rot[b].rearrange("(t p) h d -> p t (h d)", p=P),
+            )
+            v_sb = raw_pool.tile([P, 4 * KV * HD], BF16)
+            nc.sync.dma_start(
+                out=v_sb[:].rearrange("p (u c) -> p u c", u=2),
+                in_=v[b].rearrange("(u p j) g d -> p u (j g d)", u=2, j=2),
+            )
+            x_sb = late_pool.tile([P, TILES * D], BF16)
+            nc.sync.dma_start(
+                out=x_sb[:].rearrange("p (t d) -> p t d", t=TILES),
+                in_=x[b].rearrange("(t p) d -> p t d", p=P),
+            )
+            raw_of[b] = (k_sb, q_sb, v_sb)
+            x_of[b] = x_sb
+
+        def scale_k(b):
+            k_sb = raw_of[b][0]
+            nc.vector.tensor_scalar_mul(out=k_sb[:], in0=k_sb[:], scalar1=1.0 / 16.0)
+
+        def prepare_k(u):
+            k_words = raw_of[u // KV][0][:].bitcast(F32).rearrange("p (t g w) -> p t g w", t=TILES, g=KV)
+            bank = transpose_words([k_words[:, t, u % KV, :] for t in range(TILES)])
+            kT = unit_pool.tile([P, S], F32)
+            nc.scalar.copy(out=kT[:], in_=bank[:])
+            kT_of[u] = kT
+
+        def prepare_q(u, r):
+            if r == 0:
+                qT = unit_pool.tile([P, REP * S], F32)
+                qT_of[u] = qT
+            q_words = raw_of[u // KV][1][:].bitcast(F32).rearrange("p (t h w) -> p t h w", t=TILES, h=H)
+            bank = transpose_words([q_words[:, t, REP * (u % KV) + r, :] for t in range(TILES)])
+            nc.vector.tensor_copy(out=qT_of[u][:, r * S : (r + 1) * S], in_=bank[:])
+
+        def prepare_v(u):
+            v_rows = raw_of[u // KV][2][:].rearrange("p (i g d) -> p i g d", i=4, g=KV)[:, :, u % KV, :]
+            v_grouped = unit_pool.tile([P, HD * 4], BF16, align_bytes=64)
+            nc.vector.tensor_copy(
+                out=v_grouped[:].rearrange("p (c m i) -> p c i m", m=4, i=4),
+                in_=v_rows.rearrange("p i (c m) -> p c i m", m=4),
+            )
+            v_codes = long_unit_pool.tile([P, HD], U32, align_bytes=64)
+            v_scales = long_unit_pool.tile([P, HD], U8, align_bytes=64)
+            nc.vector.quantize_mx(out=v_codes[:].bitcast(FP8X4), scales=v_scales[:], in_=v_grouped[:])
+            v_of[u] = (v_codes, v_scales)
+
+        def score_tile(n, t):
+            if t == 0:
+                neg_max = stats_pool.tile([P, TILES], F32)
+                row_sum = stats_pool.tile([P, TILES], F32)
+                inv_sum = stats_pool.tile([P, TILES], F32)
+                stats_of[n] = (neg_max, row_sum, inv_sum)
+            neg_max, row_sum, inv_sum = stats_of[n]
+            u, r = n // REP, n % REP
+            kT_halves = kT_of[u][:].bitcast(BF16).rearrange("p (s j) -> p s j", j=2)
+            qT_halves = qT_of[u][:].bitcast(BF16).rearrange("p (r s j) -> p r s j", r=REP, j=2)
+            keys = (t + 1) * P
+            scores = psum_scores.tile([P, S], F32)
+            for j in range(2):
+                nc.tensor.matmul(
+                    out=scores[:, :keys],
+                    lhsT=qT_halves[:, r, t * P : (t + 1) * P, j],
+                    rhs=kT_halves[:, :keys, j],
+                    start=(j == 0),
+                    stop=False,
+                )
+            nc.tensor.matmul(
+                out=scores[:, :keys],
+                lhsT=ident_bf16[:],
+                rhs=mask_sb[:, t * S : t * S + keys],
+                start=False,
+                stop=True,
+            )
+            nc.vector.tensor_reduce(
+                out=neg_max[:, t : t + 1], in_=scores[:, :keys], axis=AXIS.X, op=ALU.max, negate=True
+            )
+            nc.scalar.activation(
+                out=e_tiles[n % E_SLOTS][t][:, :keys],
+                in_=scores[:, :keys],
+                func=ACT.Exp,
+                bias=neg_max[:, t : t + 1],
+                accum_out=row_sum[:, t : t + 1],
+            )
+            if t == TILES - 1:
+                nc.vector.reciprocal(out=inv_sum[:], in_=row_sum[:])
+
+        def transpose_e(n, pair):
+            if pair == 0:
+                e_grouped = head_pool.tile([P, S * 4], BF16, align_bytes=64)
+                e_codes = head_pool.tile([P, S], U32, align_bytes=64)
+                e_scales = head_pool.tile([P, S], U8, align_bytes=64)
+                e_mx_of[n] = (e_grouped, e_codes, e_scales)
+            e_set = e_tiles[n % E_SLOTS]
+            bank = transpose_words(
+                [e_set[2 * pair + a][:].bitcast(F32)[:, u * P : (u + 1) * P] for a in range(2) for u in range(2)]
+            )
+            interleave(nc.scalar.copy, e_mx_of[n][0][:].bitcast(F32)[:, pair * 4 * P : (pair + 1) * 4 * P], bank)
+
+        def quantise_e(n):
+            e_grouped, e_codes, e_scales = e_mx_of[n]
+            nc.vector.quantize_mx(out=e_codes[:].bitcast(FP8X4), scales=e_scales[:], in_=e_grouped[:])
+
+        def e_times_v(n, pair):
+            u, r = n // REP, n % REP
+            if r == 0 and pair == 0:
+                o_sb = unit_pool.tile([P, TILES * REP * HD], BF16)
+                o_of[u] = o_sb
+            e_codes, e_scales = e_mx_of[n][1], e_mx_of[n][2]
+            v_codes, v_scales = v_of[u]
+            inv_sum = stats_of[n][2]
+            pv = psum_mx.tile([P, 2 * HD], F32, tag="mx")
+            for a in range(2):
+                t = 2 * pair + a
+                nc.tensor.matmul_mx(
+                    out=pv[:, a * HD : (a + 1) * HD],
+                    lhsT=e_codes[:, t * P : (t + 1) * P].bitcast(FP8X4),
+                    lhsT_scale=e_scales[:, t * P : (t + 1) * P],
+                    rhs=v_codes[:].bitcast(FP8X4),
+                    rhs_scale=v_scales[:],
+                    start=True,
+                    stop=True,
+                )
+            for a in range(2):
+                t = 2 * pair + a
+                nc.scalar.activation(
+                    out=o_of[u][:, (t * REP + r) * HD : (t * REP + r + 1) * HD],
+                    in_=pv[:, a * HD : (a + 1) * HD],
+                    func=ACT.Copy,
+                    scale=inv_sum[:, t : t + 1],
+                )
+
+        def transpose_o(u, pair):
+            if pair == 0:
+                o_grouped = unit_pool.tile([P, S * 4], BF16, align_bytes=64)
+                o_codes = long_unit_pool.tile([P, S], U32, align_bytes=64)
+                o_scales = long_unit_pool.tile([P, S], U8, align_bytes=64)
+                o_mx_of[u] = (o_grouped, o_codes, o_scales)
+            o_words = o_of[u][:].bitcast(F32).rearrange("p (t r w) -> p t r w", t=TILES, r=REP)
+            bank = transpose_words([o_words[:, 2 * pair + a, r, :] for a in range(2) for r in range(REP)])
+            interleave(
+                nc.vector.tensor_copy, o_mx_of[u][0][:].bitcast(F32)[:, pair * 4 * P : (pair + 1) * 4 * P], bank
+            )
+
+        def quantise_o(u):
+            o_grouped, o_codes, o_scales = o_mx_of[u]
+            nc.vector.quantize_mx(out=o_codes[:].bitcast(FP8X4), scales=o_scales[:], in_=o_grouped[:])
+
+        def project(b, pair):
+            if pair == 0:
+                out_sb = late_pool.tile([P, TILES * D], F32)
+                out_of[b] = out_sb
+            proj = psum_mx.tile([P, 2 * D], F32, tag="mx")
+            for a in range(2):
+                t = 2 * pair + a
+                for g in range(KV):
+                    o_codes, o_scales = o_mx_of[KV * b + g][1], o_mx_of[KV * b + g][2]
+                    nc.tensor.matmul_mx(
+                        out=proj[:, a * D : (a + 1) * D],
+                        lhsT=o_codes[:, t * P : (t + 1) * P].bitcast(FP8X4),
+                        lhsT_scale=o_scales[:, t * P : (t + 1) * P],
+                        rhs=wo_codes[:, g * D : (g + 1) * D].bitcast(FP8X4),
+                        rhs_scale=wo_scales[:, g * D : (g + 1) * D],
+                        start=(g == 0),
+                        stop=(g == KV - 1),
+                    )
+            nc.vector.tensor_tensor(
+                out=out_of[b][:, pair * 2 * D : (pair + 1) * 2 * D],
+                in0=proj[:],
+                in1=x_of[b][:, pair * 2 * D : (pair + 1) * 2 * D],
+                op=ALU.add,
+            )
+            if pair == 1:
+                nc.sync.dma_start(
+                    out=out[b].rearrange("(t p) d -> p t d", p=P),
+                    in_=out_of[b][:].rearrange("p (t d) -> p t d", t=TILES),
+                )
+
+        load(0)
         nc.sync.dma_start(
             out=mask_sb[:].rearrange("p (t k) -> p t k", t=TILES),
             in_=mask.rearrange("(t p) k -> p t k", p=P),
         )
-
         wo_sb = fixed.tile([P, (D // P) * NQ], BF16)
         nc.sync.dma_start(
             out=wo_sb[:].rearrange("p (t j) -> p t j", t=D // P),
             in_=wo.rearrange("(t p) j -> p t j", p=P),
         )
-        wo_words = wo_sb[:].bitcast(F32).rearrange("p (t h w) -> p t h w", t=D // P, h=H)
-        wo_grouped = fixed.tile([P, KV * D * 4], BF16, align_bytes=64)
-        wo_codes = fixed.tile([P, KV * D], U32, align_bytes=64)
-        wo_scales = fixed.tile([P, KV * D], U8, align_bytes=64)
-        for g in range(KV):
-            bank = psum_t.tile([P, 4 * P], F32, tag="bank")
-            transpose_words(bank, [wo_words[:, t, REP * g + u, :] for t in range(D // P) for u in range(REP)])
-            interleave(
-                nc.vector.tensor_copy,
-                wo_grouped[:].bitcast(F32)[:, g * 2 * D : (g + 1) * 2 * D],
-                bank[:],
-            )
-        nc.vector.quantize_mx(out=wo_codes[:].bitcast(FP8X4), scales=wo_scales[:], in_=wo_grouped[:])
 
         e_tiles = [
             [fixed.tile([P, S], BF16, name="e_%d_%d" % (slot, t)) for t in range(TILES)]
@@ -80,175 +264,66 @@ def tile_transformerblock_pb_t_kernel(tc, q_rot, k_rot, v, mask, wo, x, out):
             for t in range(TILES - 1):
                 nc.vector.memset(e_tiles[slot][t][:, (t + 1) * P :], 0.0)
 
-        for b in range(B):
-            k_sb = batch.tile([P, TILES * KV * HD], BF16)
-            nc.sync.dma_start(
-                out=k_sb[:].rearrange("p (t c) -> p t c", t=TILES),
-                in_=k_rot[b].rearrange("(t p) g d -> p t (g d)", p=P),
-            )
-            q_sb = batch.tile([P, TILES * NQ], BF16)
-            nc.sync.dma_start(
-                out=q_sb[:].rearrange("p (t c) -> p t c", t=TILES),
-                in_=q_rot[b].rearrange("(t p) h d -> p t (h d)", p=P),
-            )
-            v_sb = batch.tile([P, 4 * KV * HD], BF16)
-            nc.sync.dma_start(
-                out=v_sb[:].rearrange("p (u c) -> p u c", u=2),
-                in_=v[b].rearrange("(u p j) g d -> p u (j g d)", u=2, j=2),
-            )
-            x_sb = batch.tile([P, TILES * D], BF16)
-            nc.sync.dma_start(
-                out=x_sb[:].rearrange("p (t d) -> p t d", t=TILES),
-                in_=x[b].rearrange("(t p) d -> p t d", p=P),
-            )
+        scale_k(0)
+        prepare_k(0)
+        prepare_q(0, 0)
+        prepare_q(0, 1)
+        prepare_v(0)
 
-            v_grouped = batch.tile([P, KV * HD * 4], BF16, align_bytes=64)
-            nc.vector.tensor_copy(
-                out=v_grouped[:].rearrange("p (c i) -> p c i", i=4),
-                in_=v_sb[:].rearrange("p (i c) -> p c i", i=4),
-            )
-            v_codes = batch.tile([P, KV * HD], U32, align_bytes=64)
-            v_scales = batch.tile([P, KV * HD], U8, align_bytes=64)
-            nc.vector.quantize_mx(out=v_codes[:].bitcast(FP8X4), scales=v_scales[:], in_=v_grouped[:])
+        wo_words = wo_sb[:].bitcast(F32).rearrange("p (t h w) -> p t h w", t=D // P, h=H)
+        wo_grouped = fixed.tile([P, KV * D * 4], BF16, align_bytes=64)
+        wo_codes = fixed.tile([P, KV * D], U32, align_bytes=64)
+        wo_scales = fixed.tile([P, KV * D], U8, align_bytes=64)
+        for g in range(KV):
+            bank = transpose_words([wo_words[:, t, REP * g + u, :] for t in range(D // P) for u in range(REP)])
+            interleave(nc.vector.tensor_copy, wo_grouped[:].bitcast(F32)[:, g * 2 * D : (g + 1) * 2 * D], bank)
+        nc.vector.quantize_mx(out=wo_codes[:].bitcast(FP8X4), scales=wo_scales[:], in_=wo_grouped[:])
 
-            nc.vector.tensor_scalar_mul(out=k_sb[:], in0=k_sb[:], scalar1=1.0 / 16.0)
-            k_words = k_sb[:].bitcast(F32).rearrange("p (t g w) -> p t g w", t=TILES, g=KV)
-            q_words = q_sb[:].bitcast(F32).rearrange("p (t h w) -> p t h w", t=TILES, h=H)
-            kT = batch.tile([P, KV * S], F32)
-            qT = batch.tile([P, H * S], F32)
-            for g in range(KV):
-                bank = psum_t.tile([P, 4 * P], F32, tag="bank")
-                transpose_words(bank, [k_words[:, t, g, :] for t in range(TILES)])
-                nc.vector.tensor_copy(out=kT[:, g * S : (g + 1) * S], in_=bank[:])
-            for t in range(TILES):
-                bank = psum_t.tile([P, 4 * P], F32, tag="bank")
-                transpose_words(bank, [q_words[:, t, h, :] for h in range(H)])
-                nc.vector.tensor_copy(
-                    out=qT[:].rearrange("p (h s) -> p h s", h=H)[:, :, t * P : (t + 1) * P],
-                    in_=bank[:].rearrange("p (h s) -> p h s", h=H),
-                )
-            kT_halves = kT[:].bitcast(BF16).rearrange("p (g s j) -> p g s j", g=KV, j=2)
-            qT_halves = qT[:].bitcast(BF16).rearrange("p (h s j) -> p h s j", h=H, j=2)
+        for n in range(HEADS + 4):
+            b, h = n // H, n % H
+            u, r = n // REP, n % REP
+            first_of_unit, last_of_unit = r == 0, r == REP - 1
 
-            o_sb = batch.tile([P, TILES * NQ], BF16)
-            for h in range(H):
-                g = h // REP
-                e_set = e_tiles[h % E_SLOTS]
-                neg_max = head.tile([P, TILES], F32)
-                row_sum = head.tile([P, TILES], F32)
-                for t in range(TILES):
-                    keys = (t + 1) * P
-                    scores = psum_s.tile([P, S], F32)
-                    for j in range(2):
-                        nc.tensor.matmul(
-                            out=scores[:, :keys],
-                            lhsT=qT_halves[:, h, t * P : (t + 1) * P, j],
-                            rhs=kT_halves[:, g, :keys, j],
-                            start=(j == 0),
-                            stop=False,
-                        )
-                    nc.tensor.matmul(
-                        out=scores[:, :keys],
-                        lhsT=ident_bf16[:],
-                        rhs=mask_sb[:, t * S : t * S + keys],
-                        start=False,
-                        stop=True,
-                    )
-                    nc.vector.tensor_reduce(
-                        out=neg_max[:, t : t + 1], in_=scores[:, :keys], axis=AXIS.X, op=ALU.max, negate=True
-                    )
-                    nc.scalar.activation(
-                        out=e_set[t][:, :keys],
-                        in_=scores[:, :keys],
-                        func=ACT.Exp,
-                        bias=neg_max[:, t : t + 1],
-                        accum_out=row_sum[:, t : t + 1],
-                    )
-                inv_sum = head.tile([P, TILES], F32)
-                nc.vector.reciprocal(out=inv_sum[:], in_=row_sum[:])
+            if h == 0 and b + 1 < B:
+                load(b + 1)
+            if 0 <= n - 1 < HEADS:
+                transpose_e(n - 1, 0)
+            if first_of_unit and 0 <= u - 2 < UNITS:
+                transpose_o(u - 2, 0)
+            if last_of_unit and u + 1 < UNITS:
+                prepare_k(u + 1)
+            if n < HEADS:
+                score_tile(n, 0)
 
-                e_grouped = head.tile([P, S * 4], BF16, align_bytes=64)
-                for pair in range(TILES // 2):
-                    bank = psum_t.tile([P, 4 * P], F32, tag="bank")
-                    transpose_words(
-                        bank,
-                        [
-                            e_set[2 * pair + a][:].bitcast(F32)[:, u * P : (u + 1) * P]
-                            for a in range(2)
-                            for u in range(2)
-                        ],
-                    )
-                    interleave(
-                        nc.scalar.copy,
-                        e_grouped[:].bitcast(F32)[:, pair * 4 * P : (pair + 1) * 4 * P],
-                        bank[:],
-                    )
-                e_codes = head.tile([P, S], U32, align_bytes=64)
-                e_scales = head.tile([P, S], U8, align_bytes=64)
-                nc.vector.quantize_mx(out=e_codes[:].bitcast(FP8X4), scales=e_scales[:], in_=e_grouped[:])
+            if 0 <= n - 1 < HEADS:
+                transpose_e(n - 1, 1)
+            if first_of_unit and 0 <= u - 2 < UNITS:
+                transpose_o(u - 2, 1)
+            if last_of_unit and u + 1 < UNITS:
+                prepare_q(u + 1, 0)
+                prepare_q(u + 1, 1)
+            if n < HEADS:
+                score_tile(n, 1)
 
-                for pair in range(TILES // 2):
-                    pv = psum_pv.tile([P, 2 * HD], F32)
-                    for a in range(2):
-                        t = 2 * pair + a
-                        nc.tensor.matmul_mx(
-                            out=pv[:, a * HD : (a + 1) * HD],
-                            lhsT=e_codes[:, t * P : (t + 1) * P].bitcast(FP8X4),
-                            lhsT_scale=e_scales[:, t * P : (t + 1) * P],
-                            rhs=v_codes[:, g * HD : (g + 1) * HD].bitcast(FP8X4),
-                            rhs_scale=v_scales[:, g * HD : (g + 1) * HD],
-                            start=True,
-                            stop=True,
-                        )
-                    for a in range(2):
-                        t = 2 * pair + a
-                        nc.scalar.activation(
-                            out=o_sb[:, t * NQ + h * HD : t * NQ + (h + 1) * HD],
-                            in_=pv[:, a * HD : (a + 1) * HD],
-                            func=ACT.Copy,
-                            scale=inv_sum[:, t : t + 1],
-                        )
+            if 0 <= n - 2 < HEADS:
+                e_times_v(n - 2, 0)
+            if h == H - 1 and b >= 1:
+                project(b - 1, 0)
+            if n < HEADS:
+                score_tile(n, 2)
 
-            o_words = o_sb[:].bitcast(F32).rearrange("p (t h w) -> p t h w", t=TILES, h=H)
-            o_grouped = batch.tile([P, KV * S * 4], BF16, align_bytes=64)
-            o_codes = batch.tile([P, KV * S], U32, align_bytes=64)
-            o_scales = batch.tile([P, KV * S], U8, align_bytes=64)
-            for g in range(KV):
-                for pair in range(TILES // 2):
-                    bank = psum_t.tile([P, 4 * P], F32, tag="bank")
-                    transpose_words(
-                        bank, [o_words[:, 2 * pair + a, REP * g + u, :] for a in range(2) for u in range(REP)]
-                    )
-                    first = (g * S + pair * 2 * P) * 2
-                    interleave(nc.vector.tensor_copy, o_grouped[:].bitcast(F32)[:, first : first + 4 * P], bank[:])
-                nc.vector.quantize_mx(
-                    out=o_codes[:, g * S : (g + 1) * S].bitcast(FP8X4),
-                    scales=o_scales[:, g * S : (g + 1) * S],
-                    in_=o_grouped[:, g * S * 4 : (g + 1) * S * 4],
-                )
+            if 0 <= n - 2 < HEADS:
+                e_times_v(n - 2, 1)
+            if h == H - 1 and b >= 1:
+                project(b - 1, 1)
+            if n < HEADS:
+                score_tile(n, 3)
 
-            out_sb = batch.tile([P, TILES * D], F32)
-            for pair in range(TILES // 2):
-                proj = psum_out.tile([P, 2 * D], F32)
-                for a in range(2):
-                    t = 2 * pair + a
-                    for g in range(KV):
-                        nc.tensor.matmul_mx(
-                            out=proj[:, a * D : (a + 1) * D],
-                            lhsT=o_codes[:, g * S + t * P : g * S + (t + 1) * P].bitcast(FP8X4),
-                            lhsT_scale=o_scales[:, g * S + t * P : g * S + (t + 1) * P],
-                            rhs=wo_codes[:, g * D : (g + 1) * D].bitcast(FP8X4),
-                            rhs_scale=wo_scales[:, g * D : (g + 1) * D],
-                            start=(g == 0),
-                            stop=(g == KV - 1),
-                        )
-                nc.vector.tensor_tensor(
-                    out=out_sb[:, pair * 2 * D : (pair + 1) * 2 * D],
-                    in0=proj[:],
-                    in1=x_sb[:, pair * 2 * D : (pair + 1) * 2 * D],
-                    op=ALU.add,
-                )
-            nc.sync.dma_start(
-                out=out[b].rearrange("(t p) d -> p t d", p=P),
-                in_=out_sb[:].rearrange("p (t d) -> p t d", t=TILES),
-            )
+            if 0 <= n - 1 < HEADS:
+                quantise_e(n - 1)
+            if first_of_unit and 0 <= u - 2 < UNITS:
+                quantise_o(u - 2)
+            if last_of_unit and u + 1 < UNITS:
+                prepare_v(u + 1)
+            if h == H - 2 and b + 1 < B:
+                scale_k(b + 1)

@@ -18,6 +18,7 @@ TILES = S // P
 WORDS = HD // 2
 E_SLOTS = 2
 HEADS = B * H
+PSUM_BANKS = 8
 UNITS = B * KV
 
 FLOPS = 2 * B * H * S * S * HD * 2 + 2 * B * S * NQ * D
@@ -33,9 +34,8 @@ def tile_transformerblock_pb_t_kernel(tc, q_rot, k_rot, v, mask, wo, x, out):
         tc.tile_pool(name="long_unit", bufs=4) as long_unit_pool,
         tc.tile_pool(name="head", bufs=3) as head_pool,
         tc.tile_pool(name="stats", bufs=4) as stats_pool,
-        tc.psum_pool(name="psum_scores", bufs=3) as psum_scores,
-        tc.psum_pool(name="psum_words", bufs=3) as psum_words,
-        tc.psum_pool(name="psum_mx", bufs=2) as psum_mx,
+        tc.psum_pool(name="psum", bufs=PSUM_BANKS) as psum,
+        tc.manual_schedule(),
     ):
         ident_f32 = fixed.tile([P, P], F32)
         make_identity(nc, ident_f32[:])
@@ -43,7 +43,7 @@ def tile_transformerblock_pb_t_kernel(tc, q_rot, k_rot, v, mask, wo, x, out):
         make_identity(nc, ident_bf16[:])
 
         def transpose_words(sources):
-            bank = psum_words.tile([P, 4 * P], F32)
+            bank = psum.tile([P, 4 * P], F32, tag="bank")
             for i, words in enumerate(sources):
                 nc.tensor.transpose(bank[:, i * P : (i + 1) * P], words, ident_f32[:])
             return bank
@@ -115,17 +115,17 @@ def tile_transformerblock_pb_t_kernel(tc, q_rot, k_rot, v, mask, wo, x, out):
             v_of[u] = (v_codes, v_scales)
 
         def score_tile(n, t):
-            if t == 0:
+            if t == TILES - 1:
                 neg_max = stats_pool.tile([P, TILES], F32)
                 row_sum = stats_pool.tile([P, TILES], F32)
                 inv_sum = stats_pool.tile([P, TILES], F32)
                 stats_of[n] = (neg_max, row_sum, inv_sum)
-            neg_max, row_sum, inv_sum = stats_of[n]
+            neg_max, row_sum = stats_of[n][0], stats_of[n][1]
             u, r = n // REP, n % REP
             kT_halves = kT_of[u][:].bitcast(BF16).rearrange("p (s j) -> p s j", j=2)
             qT_halves = qT_of[u][:].bitcast(BF16).rearrange("p (r s j) -> p r s j", r=REP, j=2)
             keys = (t + 1) * P
-            scores = psum_scores.tile([P, S], F32)
+            scores = psum.tile([P, S], F32, tag="bank")
             for j in range(2):
                 nc.tensor.matmul(
                     out=scores[:, :keys],
@@ -151,11 +151,9 @@ def tile_transformerblock_pb_t_kernel(tc, q_rot, k_rot, v, mask, wo, x, out):
                 bias=neg_max[:, t : t + 1],
                 accum_out=row_sum[:, t : t + 1],
             )
-            if t == TILES - 1:
-                nc.vector.reciprocal(out=inv_sum[:], in_=row_sum[:])
 
         def transpose_e(n, pair):
-            if pair == 0:
+            if pair == 1:
                 e_grouped = head_pool.tile([P, S * 4], BF16, align_bytes=64)
                 e_codes = head_pool.tile([P, S], U32, align_bytes=64)
                 e_scales = head_pool.tile([P, S], U8, align_bytes=64)
@@ -169,6 +167,8 @@ def tile_transformerblock_pb_t_kernel(tc, q_rot, k_rot, v, mask, wo, x, out):
         def quantise_e(n):
             e_grouped, e_codes, e_scales = e_mx_of[n]
             nc.vector.quantize_mx(out=e_codes[:].bitcast(FP8X4), scales=e_scales[:], in_=e_grouped[:])
+            row_sum, inv_sum = stats_of[n][1], stats_of[n][2]
+            nc.vector.reciprocal(out=inv_sum[:], in_=row_sum[:])
 
         def e_times_v(n, pair):
             u, r = n // REP, n % REP
@@ -178,7 +178,7 @@ def tile_transformerblock_pb_t_kernel(tc, q_rot, k_rot, v, mask, wo, x, out):
             e_codes, e_scales = e_mx_of[n][1], e_mx_of[n][2]
             v_codes, v_scales = v_of[u]
             inv_sum = stats_of[n][2]
-            pv = psum_mx.tile([P, 2 * HD], F32, tag="mx")
+            pv = psum.tile([P, 2 * HD], F32, tag="bank")
             for a in range(2):
                 t = 2 * pair + a
                 nc.tensor.matmul_mx(
@@ -219,7 +219,7 @@ def tile_transformerblock_pb_t_kernel(tc, q_rot, k_rot, v, mask, wo, x, out):
             if pair == 0:
                 out_sb = late_pool.tile([P, TILES * D], F32)
                 out_of[b] = out_sb
-            proj = psum_mx.tile([P, 2 * D], F32, tag="mx")
+            proj = psum.tile([P, 2 * D], F32, tag="bank")
             for a in range(2):
                 t = 2 * pair + a
                 for g in range(KV):
@@ -245,8 +245,65 @@ def tile_transformerblock_pb_t_kernel(tc, q_rot, k_rot, v, mask, wo, x, out):
                     in_=out_of[b][:].rearrange("p (t d) -> p t d", t=TILES),
                 )
 
+        def prepare_wo():
+            wo_words = wo_sb[:].bitcast(F32).rearrange("p (t h w) -> p t h w", t=D // P, h=H)
+            wo_grouped = fixed.tile([P, KV * D * 4], BF16, align_bytes=64)
+            for g in range(KV):
+                bank = transpose_words([wo_words[:, t, REP * g + u, :] for t in range(D // P) for u in range(REP)])
+                interleave(nc.vector.tensor_copy, wo_grouped[:].bitcast(F32)[:, g * 2 * D : (g + 1) * 2 * D], bank)
+            nc.vector.quantize_mx(out=wo_codes[:].bitcast(FP8X4), scales=wo_scales[:], in_=wo_grouped[:])
+
+        def pipeline_step(n):
+            b, h = n // H, n % H
+            u, r = n // REP, n % REP
+            first_of_unit, last_of_unit = r == 0, r == REP - 1
+
+            if h == 0 and b + 1 < B:
+                load(b + 1)
+            if 0 <= n - 1 < HEADS:
+                transpose_e(n - 1, 1)
+            if first_of_unit and 0 <= u - 2 < UNITS:
+                transpose_o(u - 2, 0)
+            if last_of_unit and u + 1 < UNITS:
+                prepare_k(u + 1)
+            if n < HEADS:
+                score_tile(n, 3)
+
+            if 0 <= n - 1 < HEADS:
+                transpose_e(n - 1, 0)
+            if first_of_unit and 0 <= u - 2 < UNITS:
+                transpose_o(u - 2, 1)
+            if last_of_unit and u + 1 < UNITS:
+                prepare_q(u + 1, 0)
+                prepare_q(u + 1, 1)
+            if n < HEADS:
+                score_tile(n, 2)
+
+            if 0 <= n - 2 < HEADS:
+                e_times_v(n - 2, 0)
+            if h == H - 1 and b >= 1:
+                project(b - 1, 0)
+            if n < HEADS:
+                score_tile(n, 1)
+
+            if 0 <= n - 2 < HEADS:
+                e_times_v(n - 2, 1)
+            if h == H - 1 and b >= 1:
+                project(b - 1, 1)
+            if n < HEADS:
+                score_tile(n, 0)
+
+            if 0 <= n - 1 < HEADS:
+                quantise_e(n - 1)
+            if first_of_unit and 0 <= u - 2 < UNITS:
+                quantise_o(u - 2)
+            if last_of_unit and u + 1 < UNITS:
+                prepare_v(u + 1)
+            if h == H - 2 and b + 1 < B:
+                scale_k(b + 1)
+
         load(0)
-        nc.sync.dma_start(
+        nc.scalar.dma_start(
             out=mask_sb[:].rearrange("p (t k) -> p t k", t=TILES),
             in_=mask.rearrange("(t p) k -> p t k", p=P),
         )
@@ -255,6 +312,8 @@ def tile_transformerblock_pb_t_kernel(tc, q_rot, k_rot, v, mask, wo, x, out):
             out=wo_sb[:].rearrange("p (t j) -> p t j", t=D // P),
             in_=wo.rearrange("(t p) j -> p t j", p=P),
         )
+        wo_codes = fixed.tile([P, KV * D], U32, align_bytes=64)
+        wo_scales = fixed.tile([P, KV * D], U8, align_bytes=64)
 
         e_tiles = [
             [fixed.tile([P, S], BF16, name="e_%d_%d" % (slot, t)) for t in range(TILES)]
@@ -270,60 +329,7 @@ def tile_transformerblock_pb_t_kernel(tc, q_rot, k_rot, v, mask, wo, x, out):
         prepare_q(0, 1)
         prepare_v(0)
 
-        wo_words = wo_sb[:].bitcast(F32).rearrange("p (t h w) -> p t h w", t=D // P, h=H)
-        wo_grouped = fixed.tile([P, KV * D * 4], BF16, align_bytes=64)
-        wo_codes = fixed.tile([P, KV * D], U32, align_bytes=64)
-        wo_scales = fixed.tile([P, KV * D], U8, align_bytes=64)
-        for g in range(KV):
-            bank = transpose_words([wo_words[:, t, REP * g + u, :] for t in range(D // P) for u in range(REP)])
-            interleave(nc.vector.tensor_copy, wo_grouped[:].bitcast(F32)[:, g * 2 * D : (g + 1) * 2 * D], bank)
-        nc.vector.quantize_mx(out=wo_codes[:].bitcast(FP8X4), scales=wo_scales[:], in_=wo_grouped[:])
-
-        for n in range(HEADS + 4):
-            b, h = n // H, n % H
-            u, r = n // REP, n % REP
-            first_of_unit, last_of_unit = r == 0, r == REP - 1
-
-            if h == 0 and b + 1 < B:
-                load(b + 1)
-            if 0 <= n - 1 < HEADS:
-                transpose_e(n - 1, 0)
-            if first_of_unit and 0 <= u - 2 < UNITS:
-                transpose_o(u - 2, 0)
-            if last_of_unit and u + 1 < UNITS:
-                prepare_k(u + 1)
-            if n < HEADS:
-                score_tile(n, 0)
-
-            if 0 <= n - 1 < HEADS:
-                transpose_e(n - 1, 1)
-            if first_of_unit and 0 <= u - 2 < UNITS:
-                transpose_o(u - 2, 1)
-            if last_of_unit and u + 1 < UNITS:
-                prepare_q(u + 1, 0)
-                prepare_q(u + 1, 1)
-            if n < HEADS:
-                score_tile(n, 1)
-
-            if 0 <= n - 2 < HEADS:
-                e_times_v(n - 2, 0)
-            if h == H - 1 and b >= 1:
-                project(b - 1, 0)
-            if n < HEADS:
-                score_tile(n, 2)
-
-            if 0 <= n - 2 < HEADS:
-                e_times_v(n - 2, 1)
-            if h == H - 1 and b >= 1:
-                project(b - 1, 1)
-            if n < HEADS:
-                score_tile(n, 3)
-
-            if 0 <= n - 1 < HEADS:
-                quantise_e(n - 1)
-            if first_of_unit and 0 <= u - 2 < UNITS:
-                quantise_o(u - 2)
-            if last_of_unit and u + 1 < UNITS:
-                prepare_v(u + 1)
-            if h == H - 2 and b + 1 < B:
-                scale_k(b + 1)
+        pipeline_step(0)
+        prepare_wo()
+        for n in range(1, HEADS + 4):
+            pipeline_step(n)

@@ -16,7 +16,7 @@ NQ = H * HD
 P = 128
 TILES = S // P
 WORDS = HD // 2
-E_SLOTS = 2
+E_SLOTS = 3
 HEADS = B * H
 PSUM_BANKS = 8
 UNITS = B * KV
@@ -29,11 +29,11 @@ def tile_transformerblock_pb_t_kernel(tc, q_rot, k_rot, v, mask, wo, x, out):
     with (
         tc.tile_pool(name="fixed", bufs=1) as fixed,
         tc.tile_pool(name="raw", bufs=2) as raw_pool,
-        tc.tile_pool(name="late", bufs=3) as late_pool,
+        tc.tile_pool(name="late", bufs=4) as late_pool,
         tc.tile_pool(name="unit", bufs=2) as unit_pool,
         tc.tile_pool(name="long_unit", bufs=4) as long_unit_pool,
         tc.tile_pool(name="head", bufs=3) as head_pool,
-        tc.tile_pool(name="stats", bufs=4) as stats_pool,
+        tc.tile_pool(name="stats", bufs=5) as stats_pool,
         tc.psum_pool(name="psum", bufs=PSUM_BANKS) as psum,
         tc.manual_schedule(),
     ):
@@ -100,7 +100,7 @@ def tile_transformerblock_pb_t_kernel(tc, q_rot, k_rot, v, mask, wo, x, out):
                 qT_of[u] = qT
             q_words = raw_of[u // KV][1][:].bitcast(F32).rearrange("p (t h w) -> p t h w", t=TILES, h=H)
             bank = transpose_words([q_words[:, t, REP * (u % KV) + r, :] for t in range(TILES)])
-            nc.vector.tensor_copy(out=qT_of[u][:, r * S : (r + 1) * S], in_=bank[:])
+            nc.scalar.copy(out=qT_of[u][:, r * S : (r + 1) * S], in_=bank[:])
 
         def prepare_v(u):
             v_rows = raw_of[u // KV][2][:].rearrange("p (i g d) -> p i g d", i=4, g=KV)[:, :, u % KV, :]
@@ -115,7 +115,7 @@ def tile_transformerblock_pb_t_kernel(tc, q_rot, k_rot, v, mask, wo, x, out):
             v_of[u] = (v_codes, v_scales)
 
         def score_tile(n, t):
-            if t == TILES - 1:
+            if t == 0:
                 neg_max = stats_pool.tile([P, TILES], F32)
                 row_sum = stats_pool.tile([P, TILES], F32)
                 inv_sum = stats_pool.tile([P, TILES], F32)
@@ -153,7 +153,7 @@ def tile_transformerblock_pb_t_kernel(tc, q_rot, k_rot, v, mask, wo, x, out):
             )
 
         def transpose_e(n, pair):
-            if pair == 1:
+            if pair == 0:
                 e_grouped = head_pool.tile([P, S * 4], BF16, align_bytes=64)
                 e_codes = head_pool.tile([P, S], U32, align_bytes=64)
                 e_scales = head_pool.tile([P, S], U8, align_bytes=64)
@@ -190,14 +190,12 @@ def tile_transformerblock_pb_t_kernel(tc, q_rot, k_rot, v, mask, wo, x, out):
                     start=True,
                     stop=True,
                 )
-            for a in range(2):
-                t = 2 * pair + a
-                nc.scalar.activation(
-                    out=o_of[u][:, (t * REP + r) * HD : (t * REP + r + 1) * HD],
-                    in_=pv[:, a * HD : (a + 1) * HD],
-                    func=ACT.Copy,
-                    scale=inv_sum[:, t : t + 1],
-                )
+            nc.vector.tensor_tensor(
+                out=o_of[u][:].rearrange("p (t r d) -> p t r d", t=TILES, r=REP)[:, 2 * pair : 2 * pair + 2, r, :],
+                in0=pv[:].rearrange("p (a d) -> p a d", a=2),
+                in1=inv_sum[:, 2 * pair : 2 * pair + 2].unsqueeze(2).to_broadcast([P, 2, HD]),
+                op=ALU.mult,
+            )
 
         def transpose_o(u, pair):
             if pair == 0:
@@ -207,9 +205,7 @@ def tile_transformerblock_pb_t_kernel(tc, q_rot, k_rot, v, mask, wo, x, out):
                 o_mx_of[u] = (o_grouped, o_codes, o_scales)
             o_words = o_of[u][:].bitcast(F32).rearrange("p (t r w) -> p t r w", t=TILES, r=REP)
             bank = transpose_words([o_words[:, 2 * pair + a, r, :] for a in range(2) for r in range(REP)])
-            interleave(
-                nc.vector.tensor_copy, o_mx_of[u][0][:].bitcast(F32)[:, pair * 4 * P : (pair + 1) * 4 * P], bank
-            )
+            interleave(nc.scalar.copy, o_mx_of[u][0][:].bitcast(F32)[:, pair * 4 * P : (pair + 1) * 4 * P], bank)
 
         def quantise_o(u):
             o_grouped, o_codes, o_scales = o_mx_of[u]
@@ -257,49 +253,52 @@ def tile_transformerblock_pb_t_kernel(tc, q_rot, k_rot, v, mask, wo, x, out):
             b, h = n // H, n % H
             u, r = n // REP, n % REP
             first_of_unit, last_of_unit = r == 0, r == REP - 1
+            transposed, multiplied = n - 2, n - 3
+            finished = u - 3
+            projected = b - 2
 
             if h == 0 and b + 1 < B:
                 load(b + 1)
-            if 0 <= n - 1 < HEADS:
-                transpose_e(n - 1, 1)
-            if first_of_unit and 0 <= u - 2 < UNITS:
-                transpose_o(u - 2, 0)
+            if 0 <= transposed < HEADS:
+                transpose_e(transposed, 0)
+            if first_of_unit and 0 <= finished < UNITS:
+                transpose_o(finished, 0)
             if last_of_unit and u + 1 < UNITS:
                 prepare_k(u + 1)
             if n < HEADS:
-                score_tile(n, 3)
+                score_tile(n, 0)
 
-            if 0 <= n - 1 < HEADS:
-                transpose_e(n - 1, 0)
-            if first_of_unit and 0 <= u - 2 < UNITS:
-                transpose_o(u - 2, 1)
+            if 0 <= transposed < HEADS:
+                transpose_e(transposed, 1)
+            if first_of_unit and 0 <= finished < UNITS:
+                transpose_o(finished, 1)
             if last_of_unit and u + 1 < UNITS:
                 prepare_q(u + 1, 0)
                 prepare_q(u + 1, 1)
             if n < HEADS:
-                score_tile(n, 2)
-
-            if 0 <= n - 2 < HEADS:
-                e_times_v(n - 2, 0)
-            if h == H - 1 and b >= 1:
-                project(b - 1, 0)
-            if n < HEADS:
                 score_tile(n, 1)
 
-            if 0 <= n - 2 < HEADS:
-                e_times_v(n - 2, 1)
-            if h == H - 1 and b >= 1:
-                project(b - 1, 1)
+            if 0 <= multiplied < HEADS:
+                e_times_v(multiplied, 0)
+            if h == 1 and 0 <= projected < B:
+                project(projected, 0)
             if n < HEADS:
-                score_tile(n, 0)
+                score_tile(n, 2)
 
-            if 0 <= n - 1 < HEADS:
-                quantise_e(n - 1)
-            if first_of_unit and 0 <= u - 2 < UNITS:
-                quantise_o(u - 2)
+            if 0 <= multiplied < HEADS:
+                e_times_v(multiplied, 1)
+            if h == 1 and 0 <= projected < B:
+                project(projected, 1)
+            if n < HEADS:
+                score_tile(n, 3)
+
+            if 0 <= transposed < HEADS:
+                quantise_e(transposed)
+            if first_of_unit and 0 <= finished < UNITS:
+                quantise_o(finished)
             if last_of_unit and u + 1 < UNITS:
                 prepare_v(u + 1)
-            if h == H - 2 and b + 1 < B:
+            if h == 1 and b + 1 < B:
                 scale_k(b + 1)
 
         load(0)
@@ -331,5 +330,5 @@ def tile_transformerblock_pb_t_kernel(tc, q_rot, k_rot, v, mask, wo, x, out):
 
         pipeline_step(0)
         prepare_wo()
-        for n in range(1, HEADS + 4):
+        for n in range(1, HEADS + 6):
             pipeline_step(n)

@@ -35,7 +35,6 @@ def tile_transformerblock_pb_t_kernel(tc, q_rot, k_rot, v, mask, wo, x, out):
         tc.tile_pool(name="head", bufs=3) as head_pool,
         tc.tile_pool(name="stats", bufs=5) as stats_pool,
         tc.psum_pool(name="psum", bufs=PSUM_BANKS) as psum,
-        tc.manual_schedule(),
     ):
         ident_f32 = fixed.tile([P, P], F32)
         make_identity(nc, ident_f32[:])
@@ -66,10 +65,16 @@ def tile_transformerblock_pb_t_kernel(tc, q_rot, k_rot, v, mask, wo, x, out):
                 in_=k_rot[b].rearrange("(t p) g d -> p t (g d)", p=P),
             )
             q_sb = raw_pool.tile([P, TILES * NQ], BF16)
-            nc.sync.dma_start(
-                out=q_sb[:].rearrange("p (t c) -> p t c", t=TILES),
-                in_=q_rot[b].rearrange("(t p) h d -> p t (h d)", p=P),
-            )
+            for g in range(KV):
+                nc.sync.dma_start(
+                    out=q_sb[:].rearrange("p (t g c) -> p t g c", t=TILES, g=KV)[:, :, g, :],
+                    in_=q_rot[b, :, REP * g : REP * (g + 1), :].rearrange("(t p) r d -> p t (r d)", p=P),
+                )
+                if b == 0 and g == 0:
+                    nc.sync.dma_start(
+                        out=mask_sb[:].rearrange("p (t k) -> p t k", t=TILES),
+                        in_=mask.rearrange("(t p) k -> p t k", p=P),
+                    )
             v_sb = raw_pool.tile([P, 4 * KV * HD], BF16)
             nc.sync.dma_start(
                 out=v_sb[:].rearrange("p (u c) -> p u c", u=2),
@@ -235,11 +240,10 @@ def tile_transformerblock_pb_t_kernel(tc, q_rot, k_rot, v, mask, wo, x, out):
                 in1=x_of[b][:, pair * 2 * D : (pair + 1) * 2 * D],
                 op=ALU.add,
             )
-            if pair == 1:
-                nc.sync.dma_start(
-                    out=out[b].rearrange("(t p) d -> p t d", p=P),
-                    in_=out_of[b][:].rearrange("p (t d) -> p t d", t=TILES),
-                )
+            nc.sync.dma_start(
+                out=out[b, pair * 2 * P : (pair + 1) * 2 * P, :].rearrange("(a p) d -> p a d", p=P),
+                in_=out_of[b][:, pair * 2 * D : (pair + 1) * 2 * D].rearrange("p (a d) -> p a d", a=2),
+            )
 
         def prepare_wo():
             wo_words = wo_sb[:].bitcast(F32).rearrange("p (t h w) -> p t h w", t=D // P, h=H)
@@ -302,10 +306,6 @@ def tile_transformerblock_pb_t_kernel(tc, q_rot, k_rot, v, mask, wo, x, out):
                 scale_k(b + 1)
 
         load(0)
-        nc.scalar.dma_start(
-            out=mask_sb[:].rearrange("p (t k) -> p t k", t=TILES),
-            in_=mask.rearrange("(t p) k -> p t k", p=P),
-        )
         wo_sb = fixed.tile([P, (D // P) * NQ], BF16)
         nc.sync.dma_start(
             out=wo_sb[:].rearrange("p (t j) -> p t j", t=D // P),
@@ -328,7 +328,10 @@ def tile_transformerblock_pb_t_kernel(tc, q_rot, k_rot, v, mask, wo, x, out):
         prepare_q(0, 1)
         prepare_v(0)
 
-        pipeline_step(0)
-        prepare_wo()
-        for n in range(1, HEADS + 6):
+        with tc.manual_schedule():
+            pipeline_step(0)
+            prepare_wo()
+            for n in range(1, HEADS):
+                pipeline_step(n)
+        for n in range(HEADS, HEADS + 6):
             pipeline_step(n)

@@ -18,8 +18,22 @@ TILES = S // P
 WORDS = HD // 2
 E_SLOTS = 3
 HEADS = B * H
-PSUM_BANKS = 8
+PSUM_BANKS = 7
 UNITS = B * KV
+
+TR_LAG = 5
+QE_LAG = 10
+INV_LAG = 9
+EV_LAG = 20
+QO_LAG = 26
+PROJ_LAG = 38
+K_LEAD = 7
+Q_LEAD = 5
+RV_LEAD = 4
+QV_LEAD = 0
+LOAD_LEAD = 16
+SCALE_LEAD = 10
+LAST_LAG = 44
 
 FLOPS = 2 * B * H * S * S * HD * 2 + 2 * B * S * NQ * D
 
@@ -33,8 +47,11 @@ def tile_transformerblock_pb_t_kernel(tc, q_rot, k_rot, v, mask, wo, x, out):
         tc.tile_pool(name="unit", bufs=2) as unit_pool,
         tc.tile_pool(name="long_unit", bufs=4) as long_unit_pool,
         tc.tile_pool(name="head", bufs=3) as head_pool,
+        tc.tile_pool(name="long_head", bufs=6) as long_head_pool,
         tc.tile_pool(name="stats", bufs=5) as stats_pool,
+        tc.tile_pool(name="inverse", bufs=3) as inverse_pool,
         tc.psum_pool(name="psum", bufs=PSUM_BANKS) as psum,
+        tc.psum_pool(name="psum_fixed", bufs=1) as psum_fixed,
     ):
         ident_f32 = fixed.tile([P, P], F32)
         make_identity(nc, ident_f32[:])
@@ -47,16 +64,10 @@ def tile_transformerblock_pb_t_kernel(tc, q_rot, k_rot, v, mask, wo, x, out):
                 nc.tensor.transpose(bank[:, i * P : (i + 1) * P], words, ident_f32[:])
             return bank
 
-        def interleave(copy, grouped_words, bank):
-            copy(
-                out=grouped_words.rearrange("p (a c u) -> p a c u", a=2, u=2),
-                in_=bank[:].rearrange("p (a u c) -> p a c u", a=2, u=2),
-            )
-
         mask_sb = fixed.tile([P, TILES * S], BF16)
 
-        raw_of, x_of, kT_of, qT_of, v_of = {}, {}, {}, {}, {}
-        stats_of, e_mx_of, o_of, o_mx_of, out_of = {}, {}, {}, {}, {}
+        raw_of, x_of, kT_of, qT_of, v_of, v_grouped_of = {}, {}, {}, {}, {}, {}
+        stats_of, inverse_of, e_mx_of, o_mx_of, out_of = {}, {}, {}, {}, {}
 
         def load(b):
             k_sb = raw_pool.tile([P, TILES * KV * HD], BF16)
@@ -90,7 +101,7 @@ def tile_transformerblock_pb_t_kernel(tc, q_rot, k_rot, v, mask, wo, x, out):
 
         def scale_k(b):
             k_sb = raw_of[b][0]
-            nc.vector.tensor_scalar_mul(out=k_sb[:], in0=k_sb[:], scalar1=1.0 / 16.0)
+            nc.gpsimd.tensor_scalar(out=k_sb[:], in0=k_sb[:], scalar1=1.0 / 16.0, scalar2=0.0, op0=ALU.mult, op1=ALU.add)
 
         def prepare_k(u):
             k_words = raw_of[u // KV][0][:].bitcast(F32).rearrange("p (t g w) -> p t g w", t=TILES, g=KV)
@@ -107,26 +118,35 @@ def tile_transformerblock_pb_t_kernel(tc, q_rot, k_rot, v, mask, wo, x, out):
             bank = transpose_words([q_words[:, t, REP * (u % KV) + r, :] for t in range(TILES)])
             nc.scalar.copy(out=qT_of[u][:, r * S : (r + 1) * S], in_=bank[:])
 
-        def prepare_v(u):
+        def regroup_v(u):
             v_rows = raw_of[u // KV][2][:].rearrange("p (i g d) -> p i g d", i=4, g=KV)[:, :, u % KV, :]
             v_grouped = unit_pool.tile([P, HD * 4], BF16, align_bytes=64)
-            nc.vector.tensor_copy(
+            nc.gpsimd.tensor_scalar(
                 out=v_grouped[:].rearrange("p (c m i) -> p c i m", m=4, i=4),
-                in_=v_rows.rearrange("p i (c m) -> p c i m", m=4),
+                in0=v_rows.rearrange("p i (c m) -> p c i m", m=4),
+                scalar1=1.0,
+                scalar2=0.0,
+                op0=ALU.mult,
+                op1=ALU.add,
             )
+            v_grouped_of[u] = v_grouped
+
+        def quantise_v(u):
+            v_grouped = v_grouped_of[u]
             v_codes = long_unit_pool.tile([P, HD], U32, align_bytes=64)
             v_scales = long_unit_pool.tile([P, HD], U8, align_bytes=64)
             nc.vector.quantize_mx(out=v_codes[:].bitcast(FP8X4), scales=v_scales[:], in_=v_grouped[:])
             v_of[u] = (v_codes, v_scales)
 
         def score_tile(n, t):
-            if t == 0:
-                neg_max = stats_pool.tile([P, TILES], F32)
-                row_sum = stats_pool.tile([P, TILES], F32)
-                inv_sum = stats_pool.tile([P, TILES], F32)
-                stats_of[n] = (neg_max, row_sum, inv_sum)
-            neg_max, row_sum = stats_of[n][0], stats_of[n][1]
             u, r = n // REP, n % REP
+            if r == 0 and t == 0:
+                neg_max = stats_pool.tile([P, TILES * REP], F32)
+                row_sum = stats_pool.tile([P, TILES * REP], F32)
+                inv_sum = stats_pool.tile([P, TILES * REP], F32)
+                stats_of[u] = (neg_max, row_sum, inv_sum)
+            neg_max, row_sum = stats_of[u][0], stats_of[u][1]
+            column = t * REP + r
             kT_halves = kT_of[u][:].bitcast(BF16).rearrange("p (s j) -> p s j", j=2)
             qT_halves = qT_of[u][:].bitcast(BF16).rearrange("p (r s j) -> p r s j", r=REP, j=2)
             keys = (t + 1) * P
@@ -147,70 +167,87 @@ def tile_transformerblock_pb_t_kernel(tc, q_rot, k_rot, v, mask, wo, x, out):
                 stop=True,
             )
             nc.vector.tensor_reduce(
-                out=neg_max[:, t : t + 1], in_=scores[:, :keys], axis=AXIS.X, op=ALU.max, negate=True
+                out=neg_max[:, column : column + 1], in_=scores[:, :keys], axis=AXIS.X, op=ALU.max, negate=True
             )
             nc.scalar.activation(
                 out=e_tiles[n % E_SLOTS][t][:, :keys],
                 in_=scores[:, :keys],
                 func=ACT.Exp,
-                bias=neg_max[:, t : t + 1],
-                accum_out=row_sum[:, t : t + 1],
+                bias=neg_max[:, column : column + 1],
+                accum_out=row_sum[:, column : column + 1],
             )
 
         def transpose_e(n, pair):
             if pair == 0:
                 e_grouped = head_pool.tile([P, S * 4], BF16, align_bytes=64)
-                e_codes = head_pool.tile([P, S], U32, align_bytes=64)
-                e_scales = head_pool.tile([P, S], U8, align_bytes=64)
+                e_codes = long_head_pool.tile([P, S], U32, align_bytes=64)
+                e_scales = long_head_pool.tile([P, S], U8, align_bytes=64)
                 e_mx_of[n] = (e_grouped, e_codes, e_scales)
             e_set = e_tiles[n % E_SLOTS]
-            bank = transpose_words(
-                [e_set[2 * pair + a][:].bitcast(F32)[:, u * P : (u + 1) * P] for a in range(2) for u in range(2)]
+            if pair == 0:
+                bank = zero_half
+            else:
+                bank = psum.tile([P, 4 * P], F32, tag="bank")
+            for u in range(1 + pair):
+                for a in range(2):
+                    words = e_set[2 * pair + a][:].bitcast(F32)[:, u * P : (u + 1) * P]
+                    nc.tensor.transpose(bank[:, (2 * u + a) * P : (2 * u + a + 1) * P], words, ident_f32[:])
+            nc.scalar.copy(
+                out=e_mx_of[n][0][:].bitcast(F32)[:, pair * 4 * P : (pair + 1) * 4 * P].rearrange("p (a c u) -> p a c u", a=2, u=2),
+                in_=bank[:].rearrange("p (u a c) -> p a c u", a=2, u=2),
             )
-            interleave(nc.scalar.copy, e_mx_of[n][0][:].bitcast(F32)[:, pair * 4 * P : (pair + 1) * 4 * P], bank)
 
         def quantise_e(n):
             e_grouped, e_codes, e_scales = e_mx_of[n]
             nc.vector.quantize_mx(out=e_codes[:].bitcast(FP8X4), scales=e_scales[:], in_=e_grouped[:])
-            row_sum, inv_sum = stats_of[n][1], stats_of[n][2]
+
+        def invert_sums(u):
+            row_sum, inv_sum = stats_of[u][1], stats_of[u][2]
             nc.vector.reciprocal(out=inv_sum[:], in_=row_sum[:])
+            spread = inverse_pool.tile([P, P * TILES * REP], F32)
+            if u == UNITS - 1:
+                for r in range(REP):
+                    bank = psum.tile([P, TILES * P], F32, tag="bank")
+                    for t in range(TILES):
+                        column = inv_sum[:, t * REP + r : t * REP + r + 1]
+                        nc.tensor.transpose(bank[:, t * P : (t + 1) * P], column.to_broadcast([P, P]), ident_f32[:])
+                    nc.scalar.copy(out=spread[:, r * TILES * P : (r + 1) * TILES * P], in_=bank[:])
+                inverse_of[u] = spread[:].rearrange("p (r t q) -> p t q r", t=TILES, r=REP)
+                return
+            inverse_of[u] = spread[:].rearrange("p (q t r) -> p t q r", t=TILES, r=REP)
+            rows = REP * TILES * P // D
+            g = u % KV
+            parked = out[u // KV, g * rows : (g + 1) * rows, :].rearrange("a d -> (a d)")
+            nc.sync.dma_start(out=parked.rearrange("(p c) -> p c", p=P), in_=inv_sum[:])
+            nc.sync.dma_start(out=spread[:], in_=parked.partition_broadcast(P))
 
-        def e_times_v(n, pair):
-            u, r = n // REP, n % REP
-            if r == 0 and pair == 0:
-                o_sb = unit_pool.tile([P, TILES * REP * HD], BF16)
-                o_of[u] = o_sb
-            e_codes, e_scales = e_mx_of[n][1], e_mx_of[n][2]
-            v_codes, v_scales = v_of[u]
-            inv_sum = stats_of[n][2]
-            pv = psum.tile([P, 2 * HD], F32, tag="bank")
-            for a in range(2):
-                t = 2 * pair + a
-                nc.tensor.matmul_mx(
-                    out=pv[:, a * HD : (a + 1) * HD],
-                    lhsT=e_codes[:, t * P : (t + 1) * P].bitcast(FP8X4),
-                    lhsT_scale=e_scales[:, t * P : (t + 1) * P],
-                    rhs=v_codes[:].bitcast(FP8X4),
-                    rhs_scale=v_scales[:],
-                    start=True,
-                    stop=True,
-                )
-            nc.vector.tensor_tensor(
-                out=o_of[u][:].rearrange("p (t r d) -> p t r d", t=TILES, r=REP)[:, 2 * pair : 2 * pair + 2, r, :],
-                in0=pv[:].rearrange("p (a d) -> p a d", a=2),
-                in1=inv_sum[:, 2 * pair : 2 * pair + 2].unsqueeze(2).to_broadcast([P, 2, HD]),
-                op=ALU.mult,
-            )
-
-        def transpose_o(u, pair):
-            if pair == 0:
+        def e_times_v(u, t):
+            if t == 0:
                 o_grouped = unit_pool.tile([P, S * 4], BF16, align_bytes=64)
                 o_codes = long_unit_pool.tile([P, S], U32, align_bytes=64)
                 o_scales = long_unit_pool.tile([P, S], U8, align_bytes=64)
                 o_mx_of[u] = (o_grouped, o_codes, o_scales)
-            o_words = o_of[u][:].bitcast(F32).rearrange("p (t r w) -> p t r w", t=TILES, r=REP)
-            bank = transpose_words([o_words[:, 2 * pair + a, r, :] for a in range(2) for r in range(REP)])
-            interleave(nc.scalar.copy, o_mx_of[u][0][:].bitcast(F32)[:, pair * 4 * P : (pair + 1) * 4 * P], bank)
+            v_codes, v_scales = v_of[u]
+            pv = psum.tile([P, 4 * P], F32, tag="bank")
+            for r in range(REP):
+                e_codes, e_scales = e_mx_of[REP * u + r][1], e_mx_of[REP * u + r][2]
+                for half in range(HD // P):
+                    i = 2 * r + half
+                    nc.tensor.matmul_mx(
+                        out=pv[:, i * P : (i + 1) * P],
+                        lhsT=v_codes[:, half * P : (half + 1) * P].bitcast(FP8X4),
+                        lhsT_scale=v_scales[:, half * P : (half + 1) * P],
+                        rhs=e_codes[:, t * P : (t + 1) * P].bitcast(FP8X4),
+                        rhs_scale=e_scales[:, t * P : (t + 1) * P],
+                        start=True,
+                        stop=True,
+                    )
+            nc.vector.tensor_tensor(
+                out=o_mx_of[u][0][:, t * 4 * P : (t + 1) * 4 * P].rearrange("p (q r h) -> p q r h", r=REP, h=2),
+                in0=pv[:].rearrange("p (r h q) -> p q r h", r=REP, h=2),
+                in1=inverse_of[u][:, t].unsqueeze(3).to_broadcast([P, P, REP, 2]),
+                op=ALU.mult,
+            )
 
         def quantise_o(u):
             o_grouped, o_codes, o_scales = o_mx_of[u]
@@ -246,64 +283,65 @@ def tile_transformerblock_pb_t_kernel(tc, q_rot, k_rot, v, mask, wo, x, out):
             )
 
         def prepare_wo():
-            wo_words = wo_sb[:].bitcast(F32).rearrange("p (t h w) -> p t h w", t=D // P, h=H)
             wo_grouped = fixed.tile([P, KV * D * 4], BF16, align_bytes=64)
             for g in range(KV):
-                bank = transpose_words([wo_words[:, t, REP * g + u, :] for t in range(D // P) for u in range(REP)])
-                interleave(nc.vector.tensor_copy, wo_grouped[:].bitcast(F32)[:, g * 2 * D : (g + 1) * 2 * D], bank)
+                bank = psum.tile([P, 4 * D], BF16, tag="bank")
+                for i in range(4):
+                    for t in range(D // P):
+                        first = t * NQ + (4 * g + i) * P
+                        nc.tensor.transpose(
+                            bank[:, i * D + t * P : i * D + (t + 1) * P], wo_sb[:, first : first + P], ident_bf16[:]
+                        )
+                nc.vector.tensor_copy(
+                    out=wo_grouped[:, g * 4 * D : (g + 1) * 4 * D].rearrange("p (c i) -> p c i", i=4),
+                    in_=bank[:].rearrange("p (i c) -> p c i", i=4),
+                )
             nc.vector.quantize_mx(out=wo_codes[:].bitcast(FP8X4), scales=wo_scales[:], in_=wo_grouped[:])
 
-        def pipeline_step(n):
-            b, h = n // H, n % H
-            u, r = n // REP, n % REP
-            first_of_unit, last_of_unit = r == 0, r == REP - 1
-            transposed, multiplied = n - 2, n - 3
-            finished = u - 3
-            projected = b - 2
-
-            if h == 0 and b + 1 < B:
-                load(b + 1)
-            if 0 <= transposed < HEADS:
-                transpose_e(transposed, 0)
-            if first_of_unit and 0 <= finished < UNITS:
-                transpose_o(finished, 0)
-            if last_of_unit and u + 1 < UNITS:
-                prepare_k(u + 1)
-            if n < HEADS:
-                score_tile(n, 0)
-
-            if 0 <= transposed < HEADS:
-                transpose_e(transposed, 1)
-            if first_of_unit and 0 <= finished < UNITS:
-                transpose_o(finished, 1)
-            if last_of_unit and u + 1 < UNITS:
-                prepare_q(u + 1, 0)
-                prepare_q(u + 1, 1)
-            if n < HEADS:
-                score_tile(n, 1)
-
-            if 0 <= multiplied < HEADS:
-                e_times_v(multiplied, 0)
-            if h == 1 and 0 <= projected < B:
-                project(projected, 0)
-            if n < HEADS:
-                score_tile(n, 2)
-
-            if 0 <= multiplied < HEADS:
-                e_times_v(multiplied, 1)
-            if h == 1 and 0 <= projected < B:
-                project(projected, 1)
-            if n < HEADS:
-                score_tile(n, 3)
-
-            if 0 <= transposed < HEADS:
-                quantise_e(transposed)
-            if first_of_unit and 0 <= finished < UNITS:
-                quantise_o(finished)
-            if last_of_unit and u + 1 < UNITS:
-                prepare_v(u + 1)
-            if h == 1 and b + 1 < B:
-                scale_k(b + 1)
+        def emit(s):
+            n, t = s // TILES, s % TILES
+            for pair in range(2):
+                m, rest = divmod(s - TR_LAG - 2 * pair, TILES)
+                if rest == 0 and 0 <= m < HEADS:
+                    transpose_e(m, pair)
+            u, rest = divmod(s + K_LEAD, REP * TILES)
+            if rest == 0 and 0 < u < UNITS:
+                prepare_k(u)
+            for r in range(REP):
+                u, rest = divmod(s + Q_LEAD - 2 * r, REP * TILES)
+                if rest == 0 and 0 < u < UNITS:
+                    prepare_q(u, r)
+            for i in range(TILES):
+                u, rest = divmod(s - EV_LAG - 2 * i, REP * TILES)
+                if rest == 0 and 0 <= u < UNITS:
+                    e_times_v(u, i)
+            for pair in range(2):
+                b, rest = divmod(s - PROJ_LAG - 4 * pair, H * TILES)
+                if rest == 0 and 0 <= b < B:
+                    project(b, pair)
+            if s < HEADS * TILES:
+                score_tile(n, t)
+            b, rest = divmod(s + LOAD_LEAD, H * TILES)
+            if rest == 0 and 0 < b < B:
+                load(b)
+            b, rest = divmod(s + SCALE_LEAD, H * TILES)
+            if rest == 0 and 0 < b < B:
+                scale_k(b)
+            m, rest = divmod(s - QE_LAG, TILES)
+            if rest == 0 and 0 <= m < HEADS:
+                quantise_e(m)
+            u, rest = divmod(s - INV_LAG, REP * TILES)
+            if rest == 0 and 0 <= u < UNITS:
+                invert_sums(u)
+            u, rest = divmod(s - QO_LAG, REP * TILES)
+            if rest == 0 and 0 <= u < UNITS:
+                quantise_o(u)
+            u, rest = divmod(s + RV_LEAD, REP * TILES)
+            if rest == 0 and 0 < u < UNITS:
+                regroup_v(u)
+            u, rest = divmod(s + QV_LEAD, REP * TILES)
+            if rest == 0 and 0 < u < UNITS:
+                quantise_v(u)
 
         load(0)
         wo_sb = fixed.tile([P, (D // P) * NQ], BF16)
@@ -322,16 +360,21 @@ def tile_transformerblock_pb_t_kernel(tc, q_rot, k_rot, v, mask, wo, x, out):
             for t in range(TILES - 1):
                 nc.vector.memset(e_tiles[slot][t][:, (t + 1) * P :], 0.0)
 
+        zero_half = psum_fixed.tile([P, 4 * P], F32)
+        for a in range(2):
+            nc.tensor.transpose(zero_half[:, (2 + a) * P : (3 + a) * P], e_tiles[0][a][:].bitcast(F32)[:, P : 2 * P], ident_f32[:])
+
         scale_k(0)
         prepare_k(0)
         prepare_q(0, 0)
         prepare_q(0, 1)
-        prepare_v(0)
+        regroup_v(0)
+        quantise_v(0)
 
         with tc.manual_schedule():
-            pipeline_step(0)
-            prepare_wo()
-            for n in range(1, HEADS):
-                pipeline_step(n)
-        for n in range(HEADS, HEADS + 6):
-            pipeline_step(n)
+            for s in range(HEADS * TILES):
+                emit(s)
+                if s == 3:
+                    prepare_wo()
+        for s in range(HEADS * TILES, HEADS * TILES + LAST_LAG):
+            emit(s)

@@ -101,7 +101,7 @@ def tile_transformerblock_pb_t_kernel(tc, q_rot, k_rot, v, mask, wo, x, out):
 
         def scale_k(b):
             k_sb = raw_of[b][0]
-            nc.gpsimd.tensor_scalar(out=k_sb[:], in0=k_sb[:], scalar1=1.0 / 16.0, scalar2=0.0, op0=ALU.mult, op1=ALU.add)
+            nc.vector.tensor_scalar_mul(out=k_sb[:], in0=k_sb[:], scalar1=1.0 / 16.0)
 
         def prepare_k(u):
             k_words = raw_of[u // KV][0][:].bitcast(F32).rearrange("p (t g w) -> p t g w", t=TILES, g=KV)
@@ -121,13 +121,9 @@ def tile_transformerblock_pb_t_kernel(tc, q_rot, k_rot, v, mask, wo, x, out):
         def regroup_v(u):
             v_rows = raw_of[u // KV][2][:].rearrange("p (i g d) -> p i g d", i=4, g=KV)[:, :, u % KV, :]
             v_grouped = unit_pool.tile([P, HD * 4], BF16, align_bytes=64)
-            nc.gpsimd.tensor_scalar(
+            nc.vector.tensor_copy(
                 out=v_grouped[:].rearrange("p (c m i) -> p c i m", m=4, i=4),
-                in0=v_rows.rearrange("p i (c m) -> p c i m", m=4),
-                scalar1=1.0,
-                scalar2=0.0,
-                op0=ALU.mult,
-                op1=ALU.add,
+                in_=v_rows.rearrange("p i (c m) -> p c i m", m=4),
             )
             v_grouped_of[u] = v_grouped
 

@@ -24,16 +24,16 @@ UNITS = B * KV
 TR_LAG = 5
 QE_LAG = 10
 INV_LAG = 9
-EV_LAG = 20
-QO_LAG = 26
-PROJ_LAG = 38
+EV_LAG = 28
+QO_LAG = 34
+PROJ_LAG = 46
 K_LEAD = 7
 Q_LEAD = 5
 RV_LEAD = 4
 QV_LEAD = 0
-LOAD_LEAD = 16
+LOAD_LEAD = 28
 SCALE_LEAD = 10
-LAST_LAG = 44
+LAST_LAG = 52
 
 FLOPS = 2 * B * H * S * S * HD * 2 + 2 * B * S * NQ * D
 
@@ -42,14 +42,14 @@ def tile_transformerblock_pb_t_kernel(tc, q_rot, k_rot, v, mask, wo, x, out):
     nc = tc.nc
     with (
         tc.tile_pool(name="fixed", bufs=1) as fixed,
-        tc.tile_pool(name="raw", bufs=2) as raw_pool,
-        tc.tile_pool(name="late", bufs=4) as late_pool,
+        tc.tile_pool(name="raw", bufs=3) as raw_pool,
+        tc.tile_pool(name="late", bufs=6) as late_pool,
         tc.tile_pool(name="unit", bufs=2) as unit_pool,
-        tc.tile_pool(name="long_unit", bufs=4) as long_unit_pool,
+        tc.tile_pool(name="long_unit", bufs=6) as long_unit_pool,
         tc.tile_pool(name="head", bufs=3) as head_pool,
-        tc.tile_pool(name="long_head", bufs=6) as long_head_pool,
+        tc.tile_pool(name="long_head", bufs=8) as long_head_pool,
         tc.tile_pool(name="stats", bufs=5) as stats_pool,
-        tc.tile_pool(name="inverse", bufs=3) as inverse_pool,
+        tc.tile_pool(name="inverse", bufs=4) as inverse_pool,
         tc.psum_pool(name="psum", bufs=PSUM_BANKS) as psum,
         tc.psum_pool(name="psum_fixed", bufs=1) as psum_fixed,
     ):
@@ -345,6 +345,9 @@ def tile_transformerblock_pb_t_kernel(tc, q_rot, k_rot, v, mask, wo, x, out):
             out=wo_sb[:].rearrange("p (t j) -> p t j", t=D // P),
             in_=wo.rearrange("(t p) j -> p t j", p=P),
         )
+        for b in range(1, B):
+            if b * H * TILES < LOAD_LEAD:
+                load(b)
         wo_codes = fixed.tile([P, KV * D], U32, align_bytes=64)
         wo_scales = fixed.tile([P, KV * D], U8, align_bytes=64)
 

@@ -21,19 +21,35 @@ HEADS = B * H
 PSUM_BANKS = 7
 UNITS = B * KV
 
-TR_LAG = 5
-QE_LAG = 10
-INV_LAG = 9
-EV_LAG = 28
-QO_LAG = 34
-PROJ_LAG = 46
-K_LEAD = 7
-Q_LEAD = 5
-RV_LEAD = 4
-QV_LEAD = 0
-LOAD_LEAD = 28
-SCALE_LEAD = 10
-LAST_LAG = 52
+COPIES = 4
+COPY_ROWS = 120
+E_A = 6
+E_B = 8
+E_C = 9
+E_D = 12
+Q_A = 0
+K_A = 2
+Q_B = 4
+V_A = 25
+V_B = 27
+V_C = 29
+V_D = 31
+PR_A = 47
+PR_B = 55
+QE_A = 12
+QE_B = 16
+INV = 9
+QO = 33
+RV_FIRST = 5
+RV = 7
+QV = 8
+SC = 1
+L_K = 2
+L_Q = 4
+L_V = 6
+L_X = 14
+WO = 20
+LAST = 180
 
 FLOPS = 2 * B * H * S * S * HD * 2 + 2 * B * S * NQ * D
 
@@ -66,46 +82,48 @@ def tile_transformerblock_pb_t_kernel(tc, q_rot, k_rot, v, mask, wo, x, out):
 
         mask_sb = fixed.tile([P, TILES * S], BF16)
 
-        raw_of, x_of, kT_of, qT_of, v_of, v_grouped_of = {}, {}, {}, {}, {}, {}
+        k_of, q_of, v_raw_of, x_of, kT_of, qT_of, v_of, v_grouped_of = {}, {}, {}, {}, {}, {}, {}, {}
         stats_of, inverse_of, e_mx_of, o_mx_of, out_of = {}, {}, {}, {}, {}
 
-        def load(b):
-            k_sb = raw_pool.tile([P, TILES * KV * HD], BF16)
+        def load_k(u):
+            k_sb = raw_pool.tile([P, TILES * HD], BF16)
             nc.sync.dma_start(
-                out=k_sb[:].rearrange("p (t c) -> p t c", t=TILES),
-                in_=k_rot[b].rearrange("(t p) g d -> p t (g d)", p=P),
+                out=k_sb[:].rearrange("p (t d) -> p t d", t=TILES),
+                in_=k_rot[u // KV, :, u % KV, :].rearrange("(t p) d -> p t d", p=P),
             )
-            q_sb = raw_pool.tile([P, TILES * NQ], BF16)
-            for g in range(KV):
-                nc.sync.dma_start(
-                    out=q_sb[:].rearrange("p (t g c) -> p t g c", t=TILES, g=KV)[:, :, g, :],
-                    in_=q_rot[b, :, REP * g : REP * (g + 1), :].rearrange("(t p) r d -> p t (r d)", p=P),
-                )
-                if b == 0 and g == 0:
-                    nc.sync.dma_start(
-                        out=mask_sb[:].rearrange("p (t k) -> p t k", t=TILES),
-                        in_=mask.rearrange("(t p) k -> p t k", p=P),
-                    )
+            k_of[u] = k_sb
+
+        def load_q(u):
+            b, g = u // KV, u % KV
+            q_sb = raw_pool.tile([P, TILES * REP * HD], BF16)
+            nc.sync.dma_start(
+                out=q_sb[:].rearrange("p (t c) -> p t c", t=TILES),
+                in_=q_rot[b, :, REP * g : REP * (g + 1), :].rearrange("(t p) r d -> p t (r d)", p=P),
+            )
+            q_of[u] = q_sb
+
+        def load_v(b):
             v_sb = raw_pool.tile([P, 4 * KV * HD], BF16)
             nc.sync.dma_start(
                 out=v_sb[:].rearrange("p (u c) -> p u c", u=2),
                 in_=v[b].rearrange("(u p j) g d -> p u (j g d)", u=2, j=2),
             )
+            v_raw_of[b] = v_sb
+
+        def load_x(b):
             x_sb = late_pool.tile([P, TILES * D], BF16)
             nc.sync.dma_start(
                 out=x_sb[:].rearrange("p (t d) -> p t d", t=TILES),
                 in_=x[b].rearrange("(t p) d -> p t d", p=P),
             )
-            raw_of[b] = (k_sb, q_sb, v_sb)
             x_of[b] = x_sb
 
-        def scale_k(b):
-            k_sb = raw_of[b][0]
-            nc.vector.tensor_scalar_mul(out=k_sb[:], in0=k_sb[:], scalar1=1.0 / 16.0)
+        def scale_k(u):
+            nc.vector.tensor_scalar_mul(out=k_of[u][:], in0=k_of[u][:], scalar1=1.0 / 16.0)
 
         def prepare_k(u):
-            k_words = raw_of[u // KV][0][:].bitcast(F32).rearrange("p (t g w) -> p t g w", t=TILES, g=KV)
-            bank = transpose_words([k_words[:, t, u % KV, :] for t in range(TILES)])
+            k_words = k_of[u][:].bitcast(F32).rearrange("p (t w) -> p t w", t=TILES)
+            bank = transpose_words([k_words[:, t, :] for t in range(TILES)])
             kT = unit_pool.tile([P, S], F32)
             nc.scalar.copy(out=kT[:], in_=bank[:])
             kT_of[u] = kT
@@ -114,12 +132,12 @@ def tile_transformerblock_pb_t_kernel(tc, q_rot, k_rot, v, mask, wo, x, out):
             if r == 0:
                 qT = unit_pool.tile([P, REP * S], F32)
                 qT_of[u] = qT
-            q_words = raw_of[u // KV][1][:].bitcast(F32).rearrange("p (t h w) -> p t h w", t=TILES, h=H)
-            bank = transpose_words([q_words[:, t, REP * (u % KV) + r, :] for t in range(TILES)])
+            q_words = q_of[u][:].bitcast(F32).rearrange("p (t r w) -> p t r w", t=TILES, r=REP)
+            bank = transpose_words([q_words[:, t, r, :] for t in range(TILES)])
             nc.scalar.copy(out=qT_of[u][:, r * S : (r + 1) * S], in_=bank[:])
 
         def regroup_v(u):
-            v_rows = raw_of[u // KV][2][:].rearrange("p (i g d) -> p i g d", i=4, g=KV)[:, :, u % KV, :]
+            v_rows = v_raw_of[u // KV][:].rearrange("p (i g d) -> p i g d", i=4, g=KV)[:, :, u % KV, :]
             v_grouped = unit_pool.tile([P, HD * 4], BF16, align_bytes=64)
             nc.vector.tensor_copy(
                 out=v_grouped[:].rearrange("p (c m i) -> p c i m", m=4, i=4),
@@ -213,9 +231,15 @@ def tile_transformerblock_pb_t_kernel(tc, q_rot, k_rot, v, mask, wo, x, out):
             inverse_of[u] = spread[:].rearrange("p (q t r) -> p t q r", t=TILES, r=REP)
             rows = REP * TILES * P // D
             g = u % KV
-            parked = out[u // KV, g * rows : (g + 1) * rows, :].rearrange("a d -> (a d)")
-            nc.sync.dma_start(out=parked.rearrange("(p c) -> p c", p=P), in_=inv_sum[:])
-            nc.sync.dma_start(out=spread[:], in_=parked.partition_broadcast(P))
+            parked = out[u // KV, : COPIES * COPY_ROWS, :].rearrange("(k s) d -> k s d", k=COPIES)
+            parked = parked[:, g * rows : (g + 1) * rows, :].rearrange("k a d -> k (a d)")
+            nc.sync.dma_start(
+                out=parked.rearrange("k (p c) -> p k c", p=P),
+                in_=inv_sum[:].unsqueeze(1).to_broadcast([P, COPIES, TILES * REP]),
+            )
+            for i in range(COPIES):
+                part = P // COPIES
+                nc.sync.dma_start(out=spread[i * part : (i + 1) * part, :], in_=parked[i].partition_broadcast(part))
 
         def e_times_v(u, t):
             if t == 0:
@@ -278,102 +302,110 @@ def tile_transformerblock_pb_t_kernel(tc, q_rot, k_rot, v, mask, wo, x, out):
                 in_=out_of[b][:, pair * 2 * D : (pair + 1) * 2 * D].rearrange("p (a d) -> p a d", a=2),
             )
 
-        def prepare_wo():
-            wo_grouped = fixed.tile([P, KV * D * 4], BF16, align_bytes=64)
-            for g in range(KV):
-                bank = psum.tile([P, 4 * D], BF16, tag="bank")
-                for i in range(4):
-                    for t in range(D // P):
-                        first = t * NQ + (4 * g + i) * P
-                        nc.tensor.transpose(
-                            bank[:, i * D + t * P : i * D + (t + 1) * P], wo_sb[:, first : first + P], ident_bf16[:]
-                        )
-                nc.vector.tensor_copy(
-                    out=wo_grouped[:, g * 4 * D : (g + 1) * 4 * D].rearrange("p (c i) -> p c i", i=4),
-                    in_=bank[:].rearrange("p (i c) -> p c i", i=4),
-                )
-            nc.vector.quantize_mx(out=wo_codes[:].bitcast(FP8X4), scales=wo_scales[:], in_=wo_grouped[:])
+        def prepare_wo(g):
+            bank = psum.tile([P, 4 * D], BF16, tag="bank")
+            for i in range(4):
+                for t in range(D // P):
+                    first = t * NQ + (4 * g + i) * P
+                    nc.tensor.transpose(
+                        bank[:, i * D + t * P : i * D + (t + 1) * P], wo_sb[:, first : first + P], ident_bf16[:]
+                    )
+            nc.vector.tensor_copy(
+                out=wo_grouped[:, g * 4 * D : (g + 1) * 4 * D].rearrange("p (c i) -> p c i", i=4),
+                in_=bank[:].rearrange("p (i c) -> p c i", i=4),
+            )
+            nc.vector.quantize_mx(
+                out=wo_codes[:, g * D : (g + 1) * D].bitcast(FP8X4),
+                scales=wo_scales[:, g * D : (g + 1) * D],
+                in_=wo_grouped[:, g * 4 * D : (g + 1) * 4 * D],
+            )
+
+        U, BE = REP * TILES, H * TILES
+        before_score = [
+            (E_A, U, UNITS, lambda u: transpose_e(2 * u, 0)),
+            (E_B, U, UNITS, lambda u: transpose_e(2 * u, 1)),
+            (E_C, U, UNITS, lambda u: transpose_e(2 * u + 1, 0)),
+            (E_D, U, UNITS, lambda u: transpose_e(2 * u + 1, 1)),
+            (Q_A, U, UNITS - 1, lambda u: prepare_q(u + 1, 0)),
+            (K_A, U, UNITS - 1, lambda u: prepare_k(u + 1)),
+            (Q_B, U, UNITS - 1, lambda u: prepare_q(u + 1, 1)),
+            (V_A, U, UNITS, lambda u: e_times_v(u, 0)),
+            (V_B, U, UNITS, lambda u: e_times_v(u, 1)),
+            (V_C, U, UNITS, lambda u: e_times_v(u, 2)),
+            (V_D, U, UNITS, lambda u: e_times_v(u, 3)),
+            (PR_A, BE, B, lambda b: project(b, 0)),
+            (PR_B, BE, B, lambda b: project(b, 1)),
+        ]
+        after_score = [
+            (QE_A, U, UNITS, lambda u: quantise_e(2 * u)),
+            (QE_B, U, UNITS, lambda u: quantise_e(2 * u + 1)),
+            (INV, U, UNITS, invert_sums),
+            (QO, U, UNITS, quantise_o),
+            (RV_FIRST, U, 1, regroup_v),
+            (RV, U, UNITS - 1, lambda u: regroup_v(u + 1)),
+            (QV, U, UNITS, quantise_v),
+            (SC, U, UNITS - 2, lambda u: scale_k(u + 2)),
+            (L_K, U, UNITS - 3, lambda u: load_k(u + 3)),
+            (L_Q, U, UNITS - 3, lambda u: load_q(u + 3)),
+            (L_V, BE, B - 1, lambda b: load_v(b + 1)),
+            (L_X, BE, B - 1, lambda b: load_x(b + 1)),
+            (WO, 4, D // P, prepare_wo),
+        ]
+
+        def run_due(stages, s):
+            for first, period, turns, stage in stages:
+                turn, rest = divmod(s - first, period)
+                if rest == 0 and 0 <= turn < turns:
+                    stage(turn)
 
         def emit(s):
-            n, t = s // TILES, s % TILES
-            for pair in range(2):
-                m, rest = divmod(s - TR_LAG - 2 * pair, TILES)
-                if rest == 0 and 0 <= m < HEADS:
-                    transpose_e(m, pair)
-            u, rest = divmod(s + K_LEAD, REP * TILES)
-            if rest == 0 and 0 < u < UNITS:
-                prepare_k(u)
-            for r in range(REP):
-                u, rest = divmod(s + Q_LEAD - 2 * r, REP * TILES)
-                if rest == 0 and 0 < u < UNITS:
-                    prepare_q(u, r)
-            for i in range(TILES):
-                u, rest = divmod(s - EV_LAG - 2 * i, REP * TILES)
-                if rest == 0 and 0 <= u < UNITS:
-                    e_times_v(u, i)
-            for pair in range(2):
-                b, rest = divmod(s - PROJ_LAG - 4 * pair, H * TILES)
-                if rest == 0 and 0 <= b < B:
-                    project(b, pair)
+            run_due(before_score, s)
             if s < HEADS * TILES:
-                score_tile(n, t)
-            b, rest = divmod(s + LOAD_LEAD, H * TILES)
-            if rest == 0 and 0 < b < B:
-                load(b)
-            b, rest = divmod(s + SCALE_LEAD, H * TILES)
-            if rest == 0 and 0 < b < B:
-                scale_k(b)
-            m, rest = divmod(s - QE_LAG, TILES)
-            if rest == 0 and 0 <= m < HEADS:
-                quantise_e(m)
-            u, rest = divmod(s - INV_LAG, REP * TILES)
-            if rest == 0 and 0 <= u < UNITS:
-                invert_sums(u)
-            u, rest = divmod(s - QO_LAG, REP * TILES)
-            if rest == 0 and 0 <= u < UNITS:
-                quantise_o(u)
-            u, rest = divmod(s + RV_LEAD, REP * TILES)
-            if rest == 0 and 0 < u < UNITS:
-                regroup_v(u)
-            u, rest = divmod(s + QV_LEAD, REP * TILES)
-            if rest == 0 and 0 < u < UNITS:
-                quantise_v(u)
+                score_tile(s // TILES, s % TILES)
+            run_due(after_score, s)
 
-        load(0)
+        load_k(0)
+        load_k(1)
+        load_q(0)
+        nc.sync.dma_start(
+            out=mask_sb[:].rearrange("p (t k) -> p t k", t=TILES),
+            in_=mask.rearrange("(t p) k -> p t k", p=P),
+        )
+        load_q(1)
+        load_v(0)
         wo_sb = fixed.tile([P, (D // P) * NQ], BF16)
         nc.sync.dma_start(
             out=wo_sb[:].rearrange("p (t j) -> p t j", t=D // P),
             in_=wo.rearrange("(t p) j -> p t j", p=P),
         )
-        for b in range(1, B):
-            if b * H * TILES < LOAD_LEAD:
-                load(b)
+        load_k(2)
+        load_q(2)
+        load_x(0)
+        wo_grouped = fixed.tile([P, KV * D * 4], BF16, align_bytes=64)
         wo_codes = fixed.tile([P, KV * D], U32, align_bytes=64)
         wo_scales = fixed.tile([P, KV * D], U8, align_bytes=64)
 
         e_tiles = [
-            [fixed.tile([P, S], BF16, name="e_%d_%d" % (slot, t)) for t in range(TILES)]
-            for slot in range(E_SLOTS)
+            [fixed.tile([P, S], BF16, name="e_%d_%d" % (i, t)) for t in range(TILES)]
+            for i in range(E_SLOTS)
         ]
-        for slot in range(E_SLOTS):
+        for i in range(E_SLOTS):
             for t in range(TILES - 1):
-                nc.vector.memset(e_tiles[slot][t][:, (t + 1) * P :], 0.0)
-
+                nc.vector.memset(e_tiles[i][t][:, (t + 1) * P :], 0.0)
         zero_half = psum_fixed.tile([P, 4 * P], F32)
         for a in range(2):
-            nc.tensor.transpose(zero_half[:, (2 + a) * P : (3 + a) * P], e_tiles[0][a][:].bitcast(F32)[:, P : 2 * P], ident_f32[:])
+            nc.tensor.transpose(
+                zero_half[:, (2 + a) * P : (3 + a) * P], e_tiles[0][a][:].bitcast(F32)[:, P : 2 * P], ident_f32[:]
+            )
 
         scale_k(0)
+        scale_k(1)
         prepare_k(0)
         prepare_q(0, 0)
         prepare_q(0, 1)
-        regroup_v(0)
-        quantise_v(0)
 
         with tc.manual_schedule():
             for s in range(HEADS * TILES):
                 emit(s)
-                if s == 3:
-                    prepare_wo()
-        for s in range(HEADS * TILES, HEADS * TILES + LAST_LAG):
+        for s in range(HEADS * TILES, LAST):
             emit(s)

@@ -23,33 +23,35 @@ UNITS = B * KV
 
 COPIES = 4
 COPY_ROWS = 120
-E_A = 6
-E_B = 8
-E_C = 9
-E_D = 12
-Q_A = 0
-K_A = 2
-Q_B = 4
-V_A = 25
-V_B = 27
-V_C = 29
-V_D = 31
-PR_A = 47
-PR_B = 55
-QE_A = 12
-QE_B = 16
-INV = 9
-QO = 33
-RV_FIRST = 5
-RV = 7
-QV = 8
-SC = 1
-L_K = 2
-L_Q = 4
-L_V = 6
-L_X = 14
-WO = 20
-LAST = 180
+SLOT_TILES = ((1, 0), (2,), (3,))
+GROUPS = 3
+E_A = 5
+E_B = 7
+E_C = 7
+E_D = 9
+Q_A = 1
+K_A = 3
+Q_B = 5
+V_A = 18
+V_B = 18
+V_C = 20
+V_D = 20
+PR_A = 32
+PR_B = 38
+QE_A = 8
+QE_B = 12
+INV = 7
+QO = 22
+RV_FIRST = 3
+RV = 4
+QV = 4
+SC = 4
+L_K = 1
+L_Q = 2
+L_V = 0
+L_X = 9
+WO = 14
+LAST = 150
 
 FLOPS = 2 * B * H * S * S * HD * 2 + 2 * B * S * NQ * D
 
@@ -152,44 +154,54 @@ def tile_transformerblock_pb_t_kernel(tc, q_rot, k_rot, v, mask, wo, x, out):
             nc.vector.quantize_mx(out=v_codes[:].bitcast(FP8X4), scales=v_scales[:], in_=v_grouped[:])
             v_of[u] = (v_codes, v_scales)
 
-        def score_tile(n, t):
+        def score_slot(s):
+            n, tiles = s // GROUPS, SLOT_TILES[s % GROUPS]
             u, r = n // REP, n % REP
-            if r == 0 and t == 0:
+            if r == 0 and s % GROUPS == 0:
                 neg_max = stats_pool.tile([P, TILES * REP], F32)
                 row_sum = stats_pool.tile([P, TILES * REP], F32)
                 inv_sum = stats_pool.tile([P, TILES * REP], F32)
                 stats_of[u] = (neg_max, row_sum, inv_sum)
             neg_max, row_sum = stats_of[u][0], stats_of[u][1]
-            column = t * REP + r
             kT_halves = kT_of[u][:].bitcast(BF16).rearrange("p (s j) -> p s j", j=2)
             qT_halves = qT_of[u][:].bitcast(BF16).rearrange("p (r s j) -> p r s j", r=REP, j=2)
-            keys = (t + 1) * P
-            scores = psum.tile([P, S], F32, tag="bank")
-            for j in range(2):
+            bank = psum.tile([P, S], F32, tag="bank")
+            first = 0
+            scores_of = {}
+            for t in tiles:
+                keys = (t + 1) * P
+                scores = bank[:, first : first + keys]
+                scores_of[t] = scores
+                first = first + keys
+                for j in range(2):
+                    nc.tensor.matmul(
+                        out=scores,
+                        lhsT=qT_halves[:, r, t * P : (t + 1) * P, j],
+                        rhs=kT_halves[:, :keys, j],
+                        start=(j == 0),
+                        stop=False,
+                    )
                 nc.tensor.matmul(
-                    out=scores[:, :keys],
-                    lhsT=qT_halves[:, r, t * P : (t + 1) * P, j],
-                    rhs=kT_halves[:, :keys, j],
-                    start=(j == 0),
-                    stop=False,
+                    out=scores,
+                    lhsT=ident_bf16[:],
+                    rhs=mask_sb[:, t * S : t * S + keys],
+                    start=False,
+                    stop=True,
                 )
-            nc.tensor.matmul(
-                out=scores[:, :keys],
-                lhsT=ident_bf16[:],
-                rhs=mask_sb[:, t * S : t * S + keys],
-                start=False,
-                stop=True,
-            )
-            nc.vector.tensor_reduce(
-                out=neg_max[:, column : column + 1], in_=scores[:, :keys], axis=AXIS.X, op=ALU.max, negate=True
-            )
-            nc.scalar.activation(
-                out=e_tiles[n % E_SLOTS][t][:, :keys],
-                in_=scores[:, :keys],
-                func=ACT.Exp,
-                bias=neg_max[:, column : column + 1],
-                accum_out=row_sum[:, column : column + 1],
-            )
+            for t in tiles:
+                column = t * REP + r
+                nc.vector.tensor_reduce(
+                    out=neg_max[:, column : column + 1], in_=scores_of[t], axis=AXIS.X, op=ALU.max, negate=True
+                )
+            for t in tiles:
+                column = t * REP + r
+                nc.scalar.activation(
+                    out=e_tiles[n % E_SLOTS][t][:, : (t + 1) * P],
+                    in_=scores_of[t],
+                    func=ACT.Exp,
+                    bias=neg_max[:, column : column + 1],
+                    accum_out=row_sum[:, column : column + 1],
+                )
 
         def transpose_e(n, pair):
             if pair == 0:
@@ -320,7 +332,7 @@ def tile_transformerblock_pb_t_kernel(tc, q_rot, k_rot, v, mask, wo, x, out):
                 in_=wo_grouped[:, g * 4 * D : (g + 1) * 4 * D],
             )
 
-        U, BE = REP * TILES, H * TILES
+        U, BE = REP * GROUPS, H * GROUPS
         before_score = [
             (E_A, U, UNITS, lambda u: transpose_e(2 * u, 0)),
             (E_B, U, UNITS, lambda u: transpose_e(2 * u, 1)),
@@ -349,7 +361,7 @@ def tile_transformerblock_pb_t_kernel(tc, q_rot, k_rot, v, mask, wo, x, out):
             (L_Q, U, UNITS - 3, lambda u: load_q(u + 3)),
             (L_V, BE, B - 1, lambda b: load_v(b + 1)),
             (L_X, BE, B - 1, lambda b: load_x(b + 1)),
-            (WO, 4, D // P, prepare_wo),
+            (WO, 3, D // P, prepare_wo),
         ]
 
         def run_due(stages, s):
@@ -360,8 +372,8 @@ def tile_transformerblock_pb_t_kernel(tc, q_rot, k_rot, v, mask, wo, x, out):
 
         def emit(s):
             run_due(before_score, s)
-            if s < HEADS * TILES:
-                score_tile(s // TILES, s % TILES)
+            if s < HEADS * GROUPS:
+                score_slot(s)
             run_due(after_score, s)
 
         load_k(0)
@@ -405,7 +417,7 @@ def tile_transformerblock_pb_t_kernel(tc, q_rot, k_rot, v, mask, wo, x, out):
         prepare_q(0, 1)
 
         with tc.manual_schedule():
-            for s in range(HEADS * TILES):
+            for s in range(HEADS * GROUPS):
                 emit(s)
-        for s in range(HEADS * TILES, LAST):
+        for s in range(HEADS * GROUPS, LAST):
             emit(s)

@@ -26,24 +26,24 @@ COPY_ROWS = 120
 SLOT_TILES = ((1, 0), (2,), (3,))
 GROUPS = 3
 E_A = 5
-E_B = 7
-E_C = 7
-E_D = 9
-Q_A = 1
-K_A = 3
+E_B = 8
+E_C = 8
+E_D = 11
+Q_A = 2
+K_A = 2
 Q_B = 5
-V_A = 18
-V_B = 18
-V_C = 20
-V_D = 20
-PR_A = 32
-PR_B = 38
-QE_A = 8
-QE_B = 12
+V_A = 15
+V_B = 15
+V_C = 18
+V_D = 18
+PR_A = 27
+PR_B = 33
+QE_A = 9
+QE_B = 13
 INV = 7
-QO = 22
+QO = 19
 RV_FIRST = 3
-RV = 4
+RV = 1
 QV = 4
 SC = 4
 L_K = 1

@@ -21,8 +21,8 @@ HEADS = B * H
 PSUM_BANKS = 7
 UNITS = B * KV
 
-COPIES = 4
-COPY_ROWS = 120
+COPIES = 2
+COPY_ROWS = 240
 SLOT_TILES = ((1, 0), (2,), (3,))
 GROUPS = 3
 E_A = 5
@@ -31,6 +31,7 @@ E_C = 8
 E_D = 11
 Q_A = 2
 K_A = 2
+Q_FIRST = 1
 Q_B = 5
 V_A = 15
 V_B = 15
@@ -38,13 +39,14 @@ V_C = 18
 V_D = 18
 PR_A = 27
 PR_B = 33
-QE_A = 9
+QE_A = 10
 QE_B = 13
 INV = 7
 QO = 19
 RV_FIRST = 3
 RV = 1
 QV = 4
+SC_FIRST = 0
 SC = 4
 L_K = 1
 L_Q = 2
@@ -67,6 +69,7 @@ def tile_transformerblock_pb_t_kernel(tc, q_rot, k_rot, v, mask, wo, x, out):
         tc.tile_pool(name="head", bufs=3) as head_pool,
         tc.tile_pool(name="long_head", bufs=8) as long_head_pool,
         tc.tile_pool(name="stats", bufs=5) as stats_pool,
+        tc.tile_pool(name="rows", bufs=4) as rows_pool,
         tc.tile_pool(name="inverse", bufs=4) as inverse_pool,
         tc.psum_pool(name="psum", bufs=PSUM_BANKS) as psum,
         tc.psum_pool(name="psum_fixed", bufs=1) as psum_fixed,
@@ -84,7 +87,8 @@ def tile_transformerblock_pb_t_kernel(tc, q_rot, k_rot, v, mask, wo, x, out):
 
         mask_sb = fixed.tile([P, TILES * S], BF16)
 
-        k_of, q_of, v_raw_of, x_of, kT_of, qT_of, v_of, v_grouped_of = {}, {}, {}, {}, {}, {}, {}, {}
+        k_of, q_words_of, v_raw_of, x_of, kT_of, qT_of, v_of, v_grouped_of = {}, {}, {}, {}, {}, {}, {}, {}
+        rows_of = {}
         stats_of, inverse_of, e_mx_of, o_mx_of, out_of = {}, {}, {}, {}, {}
 
         def load_k(u):
@@ -102,7 +106,17 @@ def tile_transformerblock_pb_t_kernel(tc, q_rot, k_rot, v, mask, wo, x, out):
                 out=q_sb[:].rearrange("p (t c) -> p t c", t=TILES),
                 in_=q_rot[b, :, REP * g : REP * (g + 1), :].rearrange("(t p) r d -> p t (r d)", p=P),
             )
-            q_of[u] = q_sb
+            q_words = q_sb[:].bitcast(F32).rearrange("p (t r w) -> p t r w", t=TILES, r=REP)
+            for r in range(REP):
+                q_words_of[u, r] = q_words[:, :, r, :]
+
+        def load_q_head(r):
+            q_head = fixed.tile([P, TILES * HD], BF16, name="first_q_%d" % r)
+            nc.sync.dma_start(
+                out=q_head[:].rearrange("p (t d) -> p t d", t=TILES),
+                in_=q_rot[0, :, r, :].rearrange("(t p) d -> p t d", p=P),
+            )
+            q_words_of[0, r] = q_head[:].bitcast(F32).rearrange("p (t w) -> p t w", t=TILES)
 
         def load_v(b):
             v_sb = raw_pool.tile([P, 4 * KV * HD], BF16)
@@ -134,9 +148,9 @@ def tile_transformerblock_pb_t_kernel(tc, q_rot, k_rot, v, mask, wo, x, out):
             if r == 0:
                 qT = unit_pool.tile([P, REP * S], F32)
                 qT_of[u] = qT
-            q_words = q_of[u][:].bitcast(F32).rearrange("p (t r w) -> p t r w", t=TILES, r=REP)
-            bank = transpose_words([q_words[:, t, r, :] for t in range(TILES)])
-            nc.scalar.copy(out=qT_of[u][:, r * S : (r + 1) * S], in_=bank[:])
+            bank = transpose_words([q_words_of[u, r][:, t, :] for t in range(TILES)])
+            copy = nc.vector.tensor_copy if u == 0 and r == 0 else nc.scalar.copy
+            copy(out=qT_of[u][:, r * S : (r + 1) * S], in_=bank[:])
 
         def regroup_v(u):
             v_rows = v_raw_of[u // KV][:].rearrange("p (i g d) -> p i g d", i=4, g=KV)[:, :, u % KV, :]
@@ -281,6 +295,48 @@ def tile_transformerblock_pb_t_kernel(tc, q_rot, k_rot, v, mask, wo, x, out):
                 op=ALU.mult,
             )
 
+        def rows_e_times_v(u, t):
+            if t == 0:
+                o_grouped = unit_pool.tile([P, S * 4], BF16, align_bytes=64)
+                o_codes = long_unit_pool.tile([P, S], U32, align_bytes=64)
+                o_scales = long_unit_pool.tile([P, S], U8, align_bytes=64)
+                o_mx_of[u] = (o_grouped, o_codes, o_scales)
+            v_codes, v_scales = v_of[u]
+            pv = psum.tile([P, REP * HD], F32, tag="bank")
+            o_rows = rows_pool.tile([P, REP * HD], BF16)
+            rows_of[u, t] = o_rows
+            for r in range(REP):
+                e_codes, e_scales = e_mx_of[REP * u + r][1], e_mx_of[REP * u + r][2]
+                nc.tensor.matmul_mx(
+                    out=pv[:, r * HD : (r + 1) * HD],
+                    lhsT=e_codes[:, t * P : (t + 1) * P].bitcast(FP8X4),
+                    lhsT_scale=e_scales[:, t * P : (t + 1) * P],
+                    rhs=v_codes[:].bitcast(FP8X4),
+                    rhs_scale=v_scales[:],
+                    start=True,
+                    stop=True,
+                )
+            for r in range(REP):
+                nc.scalar.activation(
+                    out=o_rows[:, r * HD : (r + 1) * HD],
+                    in_=pv[:, r * HD : (r + 1) * HD],
+                    func=ACT.Copy,
+                    scale=stats_of[u][2][:, t * REP + r : t * REP + r + 1],
+                )
+
+        def rows_transpose(u, t):
+            o_rows = rows_of[u, t]
+            bank = psum.tile([P, 4 * P], BF16, tag="bank")
+            for i in range(4):
+                nc.tensor.transpose(bank[:, i * P : (i + 1) * P], o_rows[:, i * P : (i + 1) * P], ident_bf16[:])
+            nc.scalar.copy(
+                out=o_mx_of[u][0][:, t * 4 * P : (t + 1) * 4 * P].rearrange("p (q i) -> p q i", i=4),
+                in_=bank[:].rearrange("p (i q) -> p q i", i=4),
+            )
+
+        def invert_late(u):
+            nc.vector.reciprocal(out=stats_of[u][2][:], in_=stats_of[u][1][:])
+
         def quantise_o(u):
             o_grouped, o_codes, o_scales = o_mx_of[u]
             nc.vector.quantize_mx(out=o_codes[:].bitcast(FP8X4), scales=o_scales[:], in_=o_grouped[:])
@@ -340,6 +396,7 @@ def tile_transformerblock_pb_t_kernel(tc, q_rot, k_rot, v, mask, wo, x, out):
             (E_D, U, UNITS, lambda u: transpose_e(2 * u + 1, 1)),
             (Q_A, U, UNITS - 1, lambda u: prepare_q(u + 1, 0)),
             (K_A, U, UNITS - 1, lambda u: prepare_k(u + 1)),
+            (Q_FIRST, U, 1, lambda u: prepare_q(u, 1)),
             (Q_B, U, UNITS - 1, lambda u: prepare_q(u + 1, 1)),
             (V_A, U, UNITS, lambda u: e_times_v(u, 0)),
             (V_B, U, UNITS, lambda u: e_times_v(u, 1)),
@@ -351,11 +408,13 @@ def tile_transformerblock_pb_t_kernel(tc, q_rot, k_rot, v, mask, wo, x, out):
         after_score = [
             (QE_A, U, UNITS, lambda u: quantise_e(2 * u)),
             (QE_B, U, UNITS, lambda u: quantise_e(2 * u + 1)),
-            (INV, U, UNITS, invert_sums),
+            (INV, U, UNITS - 2, invert_sums),
+            (INV + U * (UNITS - 2), 1, 1, lambda i: invert_late(UNITS - 2)),
             (QO, U, UNITS, quantise_o),
             (RV_FIRST, U, 1, regroup_v),
             (RV, U, UNITS - 1, lambda u: regroup_v(u + 1)),
             (QV, U, UNITS, quantise_v),
+            (SC_FIRST, U, 1, lambda u: scale_k(u + 1)),
             (SC, U, UNITS - 2, lambda u: scale_k(u + 2)),
             (L_K, U, UNITS - 3, lambda u: load_k(u + 3)),
             (L_Q, U, UNITS - 3, lambda u: load_q(u + 3)),
@@ -377,12 +436,13 @@ def tile_transformerblock_pb_t_kernel(tc, q_rot, k_rot, v, mask, wo, x, out):
             run_due(after_score, s)
 
         load_k(0)
-        load_k(1)
-        load_q(0)
+        load_q_head(0)
         nc.sync.dma_start(
             out=mask_sb[:].rearrange("p (t k) -> p t k", t=TILES),
             in_=mask.rearrange("(t p) k -> p t k", p=P),
         )
+        load_k(1)
+        load_q_head(1)
         load_q(1)
         load_v(0)
         wo_sb = fixed.tile([P, (D // P) * NQ], BF16)
@@ -411,13 +471,38 @@ def tile_transformerblock_pb_t_kernel(tc, q_rot, k_rot, v, mask, wo, x, out):
             )
 
         scale_k(0)
-        scale_k(1)
         prepare_k(0)
         prepare_q(0, 0)
-        prepare_q(0, 1)
 
         with tc.manual_schedule():
             for s in range(HEADS * GROUPS):
                 emit(s)
-        for s in range(HEADS * GROUPS, LAST):
-            emit(s)
+            first, late, last = UNITS - 3, UNITS - 2, UNITS - 1
+            e_times_v(first, 2)
+            e_times_v(first, 3)
+            quantise_e(2 * late + 1)
+            transpose_e(2 * last, 1)
+            transpose_e(2 * last + 1, 0)
+            transpose_e(2 * last + 1, 1)
+            invert_sums(last)
+            quantise_e(2 * last)
+            quantise_o(first)
+            rows_e_times_v(late, 0)
+            quantise_e(2 * last + 1)
+            rows_e_times_v(late, 1)
+            project(B - 2, 0)
+            e_times_v(last, 0)
+            rows_e_times_v(late, 2)
+            e_times_v(last, 1)
+            project(B - 2, 1)
+            rows_transpose(late, 0)
+            e_times_v(last, 2)
+            rows_e_times_v(late, 3)
+            e_times_v(last, 3)
+            rows_transpose(late, 1)
+            rows_transpose(late, 2)
+            rows_transpose(late, 3)
+            quantise_o(last)
+            quantise_o(late)
+            project(B - 1, 0)
+            project(B - 1, 1)

@@ -52,7 +52,7 @@ L_K = 1
 L_Q = 2
 L_V = 0
 L_X = 9
-WO = 14
+WO = 8
 LAST = 150
 
 FLOPS = 2 * B * H * S * S * HD * 2 + 2 * B * S * NQ * D
@@ -85,7 +85,7 @@ def tile_transformerblock_pb_t_kernel(tc, q_rot, k_rot, v, mask, wo, x, out):
                 nc.tensor.transpose(bank[:, i * P : (i + 1) * P], words, ident_f32[:])
             return bank
 
-        mask_sb = fixed.tile([P, TILES * S], BF16)
+        mask_of = {}
 
         k_of, q_words_of, v_raw_of, x_of, kT_of, qT_of, v_of, v_grouped_of = {}, {}, {}, {}, {}, {}, {}, {}
         rows_of = {}
@@ -180,6 +180,10 @@ def tile_transformerblock_pb_t_kernel(tc, q_rot, k_rot, v, mask, wo, x, out):
             kT_halves = kT_of[u][:].bitcast(BF16).rearrange("p (s j) -> p s j", j=2)
             qT_halves = qT_of[u][:].bitcast(BF16).rearrange("p (r s j) -> p r s j", r=REP, j=2)
             bank = psum.tile([P, S], F32, tag="bank")
+            mask_sb = mask_of[tiles]
+            nc.tensor.matmul(
+                out=bank[:, : mask_sb.shape[1]], lhsT=ident_bf16[:], rhs=mask_sb[:], start=True, stop=False
+            )
             first = 0
             scores_of = {}
             for t in tiles:
@@ -192,16 +196,9 @@ def tile_transformerblock_pb_t_kernel(tc, q_rot, k_rot, v, mask, wo, x, out):
                         out=scores,
                         lhsT=qT_halves[:, r, t * P : (t + 1) * P, j],
                         rhs=kT_halves[:, :keys, j],
-                        start=(j == 0),
-                        stop=False,
+                        start=False,
+                        stop=(j == 1 and t == tiles[-1]),
                     )
-                nc.tensor.matmul(
-                    out=scores,
-                    lhsT=ident_bf16[:],
-                    rhs=mask_sb[:, t * S : t * S + keys],
-                    start=False,
-                    stop=True,
-                )
             for t in tiles:
                 column = t * REP + r
                 nc.vector.tensor_reduce(
@@ -437,10 +434,14 @@ def tile_transformerblock_pb_t_kernel(tc, q_rot, k_rot, v, mask, wo, x, out):
 
         load_k(0)
         load_q_head(0)
-        nc.sync.dma_start(
-            out=mask_sb[:].rearrange("p (t k) -> p t k", t=TILES),
-            in_=mask.rearrange("(t p) k -> p t k", p=P),
-        )
+        for i, tiles in enumerate(SLOT_TILES):
+            mask_sb = fixed.tile([P, sum((t + 1) * P for t in tiles)], BF16, name="mask_%d" % i)
+            first = 0
+            for t in tiles:
+                keys = (t + 1) * P
+                nc.sync.dma_start(out=mask_sb[:, first : first + keys], in_=mask[t * P : (t + 1) * P, :keys])
+                first = first + keys
+            mask_of[tiles] = mask_sb
         load_k(1)
         load_q_head(1)
         load_q(1)

import concourse.mybir as mybir
from concourse.masks import make_identity

F32 = mybir.dt.float32
BF16 = mybir.dt.bfloat16
U32 = mybir.dt.uint32
U8 = mybir.dt.uint8
FP8X4 = mybir.dt.float8_e4m3fn_x4
ACT = mybir.ActivationFunctionType
ALU = mybir.AluOpType
AXIS = mybir.AxisListType

B, S, D, H, KV, HD = 8, 512, 256, 4, 2, 256
REP = H // KV
NQ = H * HD
P = 128
TILES = S // P
WORDS = HD // 2
E_SLOTS = 3
HEADS = B * H
PSUM_BANKS = 7
UNITS = B * KV

COPIES = 2
COPY_ROWS = 240
SLOT_TILES = ((1, 0), (2,), (3,))
GROUPS = 3
E_A = 5
E_B = 8
E_C = 8
E_D = 11
Q_A = 2
K_A = 2
Q_FIRST = 1
Q_B = 5
V_A = 15
V_B = 15
V_C = 18
V_D = 18
PR_A = 27
PR_B = 33
QE_A = 10
QE_B = 13
INV = 7
QO = 19
RV_FIRST = 3
RV = 1
QV = 4
SC_FIRST = 0
SC = 4
L_K = 1
L_Q = 2
L_V = 0
L_X = 9
WO = 8
LAST = 150

FLOPS = 2 * B * H * S * S * HD * 2 + 2 * B * S * NQ * D


def tile_transformerblock_pb_t_kernel(tc, q_rot, k_rot, v, mask, wo, x, out):
    nc = tc.nc
    with (
        tc.tile_pool(name="fixed", bufs=1) as fixed,
        tc.tile_pool(name="raw", bufs=3) as raw_pool,
        tc.tile_pool(name="late", bufs=6) as late_pool,
        tc.tile_pool(name="unit", bufs=2) as unit_pool,
        tc.tile_pool(name="long_unit", bufs=6) as long_unit_pool,
        tc.tile_pool(name="head", bufs=3) as head_pool,
        tc.tile_pool(name="long_head", bufs=8) as long_head_pool,
        tc.tile_pool(name="stats", bufs=5) as stats_pool,
        tc.tile_pool(name="rows", bufs=4) as rows_pool,
        tc.tile_pool(name="inverse", bufs=4) as inverse_pool,
        tc.psum_pool(name="psum", bufs=PSUM_BANKS) as psum,
        tc.psum_pool(name="psum_fixed", bufs=1) as psum_fixed,
    ):
        ident_f32 = fixed.tile([P, P], F32)
        make_identity(nc, ident_f32[:])
        ident_bf16 = fixed.tile([P, P], BF16)
        make_identity(nc, ident_bf16[:])

        def transpose_words(sources):
            bank = psum.tile([P, 4 * P], F32, tag="bank")
            for i, words in enumerate(sources):
                nc.tensor.transpose(bank[:, i * P : (i + 1) * P], words, ident_f32[:])
            return bank

        mask_of = {}

        k_of, q_words_of, v_raw_of, x_of, kT_of, qT_of, v_of, v_grouped_of = {}, {}, {}, {}, {}, {}, {}, {}
        rows_of = {}
        stats_of, inverse_of, e_mx_of, o_mx_of, out_of = {}, {}, {}, {}, {}

        def load_k(u):
            k_sb = raw_pool.tile([P, TILES * HD], BF16)
            nc.sync.dma_start(
                out=k_sb[:].rearrange("p (t d) -> p t d", t=TILES),
                in_=k_rot[u // KV, :, u % KV, :].rearrange("(t p) d -> p t d", p=P),
            )
            k_of[u] = k_sb

        def load_q(u):
            b, g = u // KV, u % KV
            q_sb = raw_pool.tile([P, TILES * REP * HD], BF16)
            nc.sync.dma_start(
                out=q_sb[:].rearrange("p (t c) -> p t c", t=TILES),
                in_=q_rot[b, :, REP * g : REP * (g + 1), :].rearrange("(t p) r d -> p t (r d)", p=P),
            )
            q_words = q_sb[:].bitcast(F32).rearrange("p (t r w) -> p t r w", t=TILES, r=REP)
            for r in range(REP):
                q_words_of[u, r] = q_words[:, :, r, :]

        def load_q_head(r):
            q_head = fixed.tile([P, TILES * HD], BF16, name="first_q_%d" % r)
            nc.sync.dma_start(
                out=q_head[:].rearrange("p (t d) -> p t d", t=TILES),
                in_=q_rot[0, :, r, :].rearrange("(t p) d -> p t d", p=P),
            )
            q_words_of[0, r] = q_head[:].bitcast(F32).rearrange("p (t w) -> p t w", t=TILES)

        def load_v(b):
            v_sb = raw_pool.tile([P, 4 * KV * HD], BF16)
            nc.sync.dma_start(
                out=v_sb[:].rearrange("p (u c) -> p u c", u=2),
                in_=v[b].rearrange("(u p j) g d -> p u (j g d)", u=2, j=2),
            )
            v_raw_of[b] = v_sb

        def load_x(b):
            x_sb = late_pool.tile([P, TILES * D], BF16)
            nc.sync.dma_start(
                out=x_sb[:].rearrange("p (t d) -> p t d", t=TILES),
                in_=x[b].rearrange("(t p) d -> p t d", p=P),
            )
            x_of[b] = x_sb

        def scale_k(u):
            nc.vector.tensor_scalar_mul(out=k_of[u][:], in0=k_of[u][:], scalar1=1.0 / 16.0)

        def prepare_k(u):
            k_words = k_of[u][:].bitcast(F32).rearrange("p (t w) -> p t w", t=TILES)
            bank = transpose_words([k_words[:, t, :] for t in range(TILES)])
            kT = unit_pool.tile([P, S], F32)
            nc.scalar.copy(out=kT[:], in_=bank[:])
            kT_of[u] = kT

        def prepare_q(u, r):
            if r == 0:
                qT = unit_pool.tile([P, REP * S], F32)
                qT_of[u] = qT
            bank = transpose_words([q_words_of[u, r][:, t, :] for t in range(TILES)])
            copy = nc.vector.tensor_copy if u == 0 and r == 0 else nc.scalar.copy
            copy(out=qT_of[u][:, r * S : (r + 1) * S], in_=bank[:])

        def regroup_v(u):
            v_rows = v_raw_of[u // KV][:].rearrange("p (i g d) -> p i g d", i=4, g=KV)[:, :, u % KV, :]
            v_grouped = unit_pool.tile([P, HD * 4], BF16, align_bytes=64)
            nc.vector.tensor_copy(
                out=v_grouped[:].rearrange("p (c m i) -> p c i m", m=4, i=4),
                in_=v_rows.rearrange("p i (c m) -> p c i m", m=4),
            )
            v_grouped_of[u] = v_grouped

        def quantise_v(u):
            v_grouped = v_grouped_of[u]
            v_codes = long_unit_pool.tile([P, HD], U32, align_bytes=64)
            v_scales = long_unit_pool.tile([P, HD], U8, align_bytes=64)
            nc.vector.quantize_mx(out=v_codes[:].bitcast(FP8X4), scales=v_scales[:], in_=v_grouped[:])
            v_of[u] = (v_codes, v_scales)

        def score_slot(s):
            n, tiles = s // GROUPS, SLOT_TILES[s % GROUPS]
            u, r = n // REP, n % REP
            if r == 0 and s % GROUPS == 0:
                neg_max = stats_pool.tile([P, TILES * REP], F32)
                row_sum = stats_pool.tile([P, TILES * REP], F32)
                inv_sum = stats_pool.tile([P, TILES * REP], F32)
                stats_of[u] = (neg_max, row_sum, inv_sum)
            neg_max, row_sum = stats_of[u][0], stats_of[u][1]
            kT_halves = kT_of[u][:].bitcast(BF16).rearrange("p (s j) -> p s j", j=2)
            qT_halves = qT_of[u][:].bitcast(BF16).rearrange("p (r s j) -> p r s j", r=REP, j=2)
            bank = psum.tile([P, S], F32, tag="bank")
            mask_sb = mask_of[tiles]
            nc.tensor.matmul(
                out=bank[:, : mask_sb.shape[1]], lhsT=ident_bf16[:], rhs=mask_sb[:], start=True, stop=False
            )
            first = 0
            scores_of = {}
            for t in tiles:
                keys = (t + 1) * P
                scores = bank[:, first : first + keys]
                scores_of[t] = scores
                first = first + keys
                for j in range(2):
                    nc.tensor.matmul(
                        out=scores,
                        lhsT=qT_halves[:, r, t * P : (t + 1) * P, j],
                        rhs=kT_halves[:, :keys, j],
                        start=False,
                        stop=(j == 1 and t == tiles[-1]),
                    )
            for t in tiles:
                column = t * REP + r
                nc.vector.tensor_reduce(
                    out=neg_max[:, column : column + 1], in_=scores_of[t], axis=AXIS.X, op=ALU.max, negate=True
                )
            for t in tiles:
                column = t * REP + r
                nc.scalar.activation(
                    out=e_tiles[n % E_SLOTS][t][:, : (t + 1) * P],
                    in_=scores_of[t],
                    func=ACT.Exp,
                    bias=neg_max[:, column : column + 1],
                    accum_out=row_sum[:, column : column + 1],
                )

        def transpose_e(n, pair):
            if pair == 0:
                e_grouped = head_pool.tile([P, S * 4], BF16, align_bytes=64)
                e_codes = long_head_pool.tile([P, S], U32, align_bytes=64)
                e_scales = long_head_pool.tile([P, S], U8, align_bytes=64)
                e_mx_of[n] = (e_grouped, e_codes, e_scales)
            e_set = e_tiles[n % E_SLOTS]
            if pair == 0:
                bank = zero_half
            else:
                bank = psum.tile([P, 4 * P], F32, tag="bank")
            for u in range(1 + pair):
                for a in range(2):
                    words = e_set[2 * pair + a][:].bitcast(F32)[:, u * P : (u + 1) * P]
                    nc.tensor.transpose(bank[:, (2 * u + a) * P : (2 * u + a + 1) * P], words, ident_f32[:])
            nc.scalar.copy(
                out=e_mx_of[n][0][:].bitcast(F32)[:, pair * 4 * P : (pair + 1) * 4 * P].rearrange("p (a c u) -> p a c u", a=2, u=2),
                in_=bank[:].rearrange("p (u a c) -> p a c u", a=2, u=2),
            )

        def quantise_e(n):
            e_grouped, e_codes, e_scales = e_mx_of[n]
            nc.vector.quantize_mx(out=e_codes[:].bitcast(FP8X4), scales=e_scales[:], in_=e_grouped[:])

        def invert_sums(u):
            row_sum, inv_sum = stats_of[u][1], stats_of[u][2]
            nc.vector.reciprocal(out=inv_sum[:], in_=row_sum[:])
            spread = inverse_pool.tile([P, P * TILES * REP], F32)
            if u == UNITS - 1:
                for r in range(REP):
                    bank = psum.tile([P, TILES * P], F32, tag="bank")
                    for t in range(TILES):
                        column = inv_sum[:, t * REP + r : t * REP + r + 1]
                        nc.tensor.transpose(bank[:, t * P : (t + 1) * P], column.to_broadcast([P, P]), ident_f32[:])
                    nc.scalar.copy(out=spread[:, r * TILES * P : (r + 1) * TILES * P], in_=bank[:])
                inverse_of[u] = spread[:].rearrange("p (r t q) -> p t q r", t=TILES, r=REP)
                return
            inverse_of[u] = spread[:].rearrange("p (q t r) -> p t q r", t=TILES, r=REP)
            rows = REP * TILES * P // D
            g = u % KV
            parked = out[u // KV, : COPIES * COPY_ROWS, :].rearrange("(k s) d -> k s d", k=COPIES)
            parked = parked[:, g * rows : (g + 1) * rows, :].rearrange("k a d -> k (a d)")
            nc.sync.dma_start(
                out=parked.rearrange("k (p c) -> p k c", p=P),
                in_=inv_sum[:].unsqueeze(1).to_broadcast([P, COPIES, TILES * REP]),
            )
            for i in range(COPIES):
                part = P // COPIES
                nc.sync.dma_start(out=spread[i * part : (i + 1) * part, :], in_=parked[i].partition_broadcast(part))

        def e_times_v(u, t):
            if t == 0:
                o_grouped = unit_pool.tile([P, S * 4], BF16, align_bytes=64)
                o_codes = long_unit_pool.tile([P, S], U32, align_bytes=64)
                o_scales = long_unit_pool.tile([P, S], U8, align_bytes=64)
                o_mx_of[u] = (o_grouped, o_codes, o_scales)
            v_codes, v_scales = v_of[u]
            pv = psum.tile([P, 4 * P], F32, tag="bank")
            for r in range(REP):
                e_codes, e_scales = e_mx_of[REP * u + r][1], e_mx_of[REP * u + r][2]
                for half in range(HD // P):
                    i = 2 * r + half
                    nc.tensor.matmul_mx(
                        out=pv[:, i * P : (i + 1) * P],
                        lhsT=v_codes[:, half * P : (half + 1) * P].bitcast(FP8X4),
                        lhsT_scale=v_scales[:, half * P : (half + 1) * P],
                        rhs=e_codes[:, t * P : (t + 1) * P].bitcast(FP8X4),
                        rhs_scale=e_scales[:, t * P : (t + 1) * P],
                        start=True,
                        stop=True,
                    )
            nc.vector.tensor_tensor(
                out=o_mx_of[u][0][:, t * 4 * P : (t + 1) * 4 * P].rearrange("p (q r h) -> p q r h", r=REP, h=2),
                in0=pv[:].rearrange("p (r h q) -> p q r h", r=REP, h=2),
                in1=inverse_of[u][:, t].unsqueeze(3).to_broadcast([P, P, REP, 2]),
                op=ALU.mult,
            )

        def rows_e_times_v(u, t):
            if t == 0:
                o_grouped = unit_pool.tile([P, S * 4], BF16, align_bytes=64)
                o_codes = long_unit_pool.tile([P, S], U32, align_bytes=64)
                o_scales = long_unit_pool.tile([P, S], U8, align_bytes=64)
                o_mx_of[u] = (o_grouped, o_codes, o_scales)
            v_codes, v_scales = v_of[u]
            pv = psum.tile([P, REP * HD], F32, tag="bank")
            o_rows = rows_pool.tile([P, REP * HD], BF16)
            rows_of[u, t] = o_rows
            for r in range(REP):
                e_codes, e_scales = e_mx_of[REP * u + r][1], e_mx_of[REP * u + r][2]
                nc.tensor.matmul_mx(
                    out=pv[:, r * HD : (r + 1) * HD],
                    lhsT=e_codes[:, t * P : (t + 1) * P].bitcast(FP8X4),
                    lhsT_scale=e_scales[:, t * P : (t + 1) * P],
                    rhs=v_codes[:].bitcast(FP8X4),
                    rhs_scale=v_scales[:],
                    start=True,
                    stop=True,
                )
            for r in range(REP):
                nc.scalar.activation(
                    out=o_rows[:, r * HD : (r + 1) * HD],
                    in_=pv[:, r * HD : (r + 1) * HD],
                    func=ACT.Copy,
                    scale=stats_of[u][2][:, t * REP + r : t * REP + r + 1],
                )

        def rows_transpose(u, t):
            o_rows = rows_of[u, t]
            bank = psum.tile([P, 4 * P], BF16, tag="bank")
            for i in range(4):
                nc.tensor.transpose(bank[:, i * P : (i + 1) * P], o_rows[:, i * P : (i + 1) * P], ident_bf16[:])
            nc.scalar.copy(
                out=o_mx_of[u][0][:, t * 4 * P : (t + 1) * 4 * P].rearrange("p (q i) -> p q i", i=4),
                in_=bank[:].rearrange("p (i q) -> p q i", i=4),
            )

        def invert_late(u):
            nc.vector.reciprocal(out=stats_of[u][2][:], in_=stats_of[u][1][:])

        def quantise_o(u):
            o_grouped, o_codes, o_scales = o_mx_of[u]
            nc.vector.quantize_mx(out=o_codes[:].bitcast(FP8X4), scales=o_scales[:], in_=o_grouped[:])

        def project(b, pair):
            if pair == 0:
                out_sb = late_pool.tile([P, TILES * D], F32)
                out_of[b] = out_sb
            proj = psum.tile([P, 2 * D], F32, tag="bank")
            for a in range(2):
                t = 2 * pair + a
                for g in range(KV):
                    o_codes, o_scales = o_mx_of[KV * b + g][1], o_mx_of[KV * b + g][2]
                    nc.tensor.matmul_mx(
                        out=proj[:, a * D : (a + 1) * D],
                        lhsT=o_codes[:, t * P : (t + 1) * P].bitcast(FP8X4),
                        lhsT_scale=o_scales[:, t * P : (t + 1) * P],
                        rhs=wo_codes[:, g * D : (g + 1) * D].bitcast(FP8X4),
                        rhs_scale=wo_scales[:, g * D : (g + 1) * D],
                        start=(g == 0),
                        stop=(g == KV - 1),
                    )
            nc.vector.tensor_tensor(
                out=out_of[b][:, pair * 2 * D : (pair + 1) * 2 * D],
                in0=proj[:],
                in1=x_of[b][:, pair * 2 * D : (pair + 1) * 2 * D],
                op=ALU.add,
            )
            nc.sync.dma_start(
                out=out[b, pair * 2 * P : (pair + 1) * 2 * P, :].rearrange("(a p) d -> p a d", p=P),
                in_=out_of[b][:, pair * 2 * D : (pair + 1) * 2 * D].rearrange("p (a d) -> p a d", a=2),
            )

        def prepare_wo(g):
            bank = psum.tile([P, 4 * D], BF16, tag="bank")
            for i in range(4):
                for t in range(D // P):
                    first = t * NQ + (4 * g + i) * P
                    nc.tensor.transpose(
                        bank[:, i * D + t * P : i * D + (t + 1) * P], wo_sb[:, first : first + P], ident_bf16[:]
                    )
            nc.vector.tensor_copy(
                out=wo_grouped[:, g * 4 * D : (g + 1) * 4 * D].rearrange("p (c i) -> p c i", i=4),
                in_=bank[:].rearrange("p (i c) -> p c i", i=4),
            )
            nc.vector.quantize_mx(
                out=wo_codes[:, g * D : (g + 1) * D].bitcast(FP8X4),
                scales=wo_scales[:, g * D : (g + 1) * D],
                in_=wo_grouped[:, g * 4 * D : (g + 1) * 4 * D],
            )

        U, BE = REP * GROUPS, H * GROUPS
        before_score = [
            (E_A, U, UNITS, lambda u: transpose_e(2 * u, 0)),
            (E_B, U, UNITS, lambda u: transpose_e(2 * u, 1)),
            (E_C, U, UNITS, lambda u: transpose_e(2 * u + 1, 0)),
            (E_D, U, UNITS, lambda u: transpose_e(2 * u + 1, 1)),
            (Q_A, U, UNITS - 1, lambda u: prepare_q(u + 1, 0)),
            (K_A, U, UNITS - 1, lambda u: prepare_k(u + 1)),
            (Q_FIRST, U, 1, lambda u: prepare_q(u, 1)),
            (Q_B, U, UNITS - 1, lambda u: prepare_q(u + 1, 1)),
            (V_A, U, UNITS, lambda u: e_times_v(u, 0)),
            (V_B, U, UNITS, lambda u: e_times_v(u, 1)),
            (V_C, U, UNITS, lambda u: e_times_v(u, 2)),
            (V_D, U, UNITS, lambda u: e_times_v(u, 3)),
            (PR_A, BE, B, lambda b: project(b, 0)),
            (PR_B, BE, B, lambda b: project(b, 1)),
        ]
        after_score = [
            (QE_A, U, UNITS, lambda u: quantise_e(2 * u)),
            (QE_B, U, UNITS, lambda u: quantise_e(2 * u + 1)),
            (INV, U, UNITS - 2, invert_sums),
            (INV + U * (UNITS - 2), 1, 1, lambda i: invert_late(UNITS - 2)),
            (QO, U, UNITS, quantise_o),
            (RV_FIRST, U, 1, regroup_v),
            (RV, U, UNITS - 1, lambda u: regroup_v(u + 1)),
            (QV, U, UNITS, quantise_v),
            (SC_FIRST, U, 1, lambda u: scale_k(u + 1)),
            (SC, U, UNITS - 2, lambda u: scale_k(u + 2)),
            (L_K, U, UNITS - 3, lambda u: load_k(u + 3)),
            (L_Q, U, UNITS - 3, lambda u: load_q(u + 3)),
            (L_V, BE, B - 1, lambda b: load_v(b + 1)),
            (L_X, BE, B - 1, lambda b: load_x(b + 1)),
            (WO, 3, D // P, prepare_wo),
        ]

        def run_due(stages, s):
            for first, period, turns, stage in stages:
                turn, rest = divmod(s - first, period)
                if rest == 0 and 0 <= turn < turns:
                    stage(turn)

        def emit(s):
            run_due(before_score, s)
            if s < HEADS * GROUPS:
                score_slot(s)
            run_due(after_score, s)

        load_k(0)
        load_q_head(0)
        for i, tiles in enumerate(SLOT_TILES):
            mask_sb = fixed.tile([P, sum((t + 1) * P for t in tiles)], BF16, name="mask_%d" % i)
            first = 0
            for t in tiles:
                keys = (t + 1) * P
                nc.sync.dma_start(out=mask_sb[:, first : first + keys], in_=mask[t * P : (t + 1) * P, :keys])
                first = first + keys
            mask_of[tiles] = mask_sb
        load_k(1)
        load_q_head(1)
        load_q(1)
        load_v(0)
        wo_sb = fixed.tile([P, (D // P) * NQ], BF16)
        nc.sync.dma_start(
            out=wo_sb[:].rearrange("p (t j) -> p t j", t=D // P),
            in_=wo.rearrange("(t p) j -> p t j", p=P),
        )
        load_k(2)
        load_q(2)
        load_x(0)
        wo_grouped = fixed.tile([P, KV * D * 4], BF16, align_bytes=64)
        wo_codes = fixed.tile([P, KV * D], U32, align_bytes=64)
        wo_scales = fixed.tile([P, KV * D], U8, align_bytes=64)

        e_tiles = [
            [fixed.tile([P, S], BF16, name="e_%d_%d" % (i, t)) for t in range(TILES)]
            for i in range(E_SLOTS)
        ]
        for i in range(E_SLOTS):
            for t in range(TILES - 1):
                nc.vector.memset(e_tiles[i][t][:, (t + 1) * P :], 0.0)
        zero_half = psum_fixed.tile([P, 4 * P], F32)
        for a in range(2):
            nc.tensor.transpose(
                zero_half[:, (2 + a) * P : (3 + a) * P], e_tiles[0][a][:].bitcast(F32)[:, P : 2 * P], ident_f32[:]
            )

        scale_k(0)
        prepare_k(0)
        prepare_q(0, 0)

        with tc.manual_schedule():
            for s in range(HEADS * GROUPS):
                emit(s)
            first, late, last = UNITS - 3, UNITS - 2, UNITS - 1
            e_times_v(first, 2)
            e_times_v(first, 3)
            quantise_e(2 * late + 1)
            transpose_e(2 * last, 1)
            transpose_e(2 * last + 1, 0)
            transpose_e(2 * last + 1, 1)
            invert_sums(last)
            quantise_e(2 * last)
            quantise_o(first)
            rows_e_times_v(late, 0)
            quantise_e(2 * last + 1)
            rows_e_times_v(late, 1)
            project(B - 2, 0)
            e_times_v(last, 0)
            rows_e_times_v(late, 2)
            e_times_v(last, 1)
            project(B - 2, 1)
            rows_transpose(late, 0)
            e_times_v(last, 2)
            rows_e_times_v(late, 3)
            e_times_v(last, 3)
            rows_transpose(late, 1)
            rows_transpose(late, 2)
            rows_transpose(late, 3)
            quantise_o(last)
            quantise_o(late)
            project(B - 1, 0)
            project(B - 1, 1)
